import numpy as np
import ml_dtypes


def mxq(x, axis, fmt="e4m3"):
    dtype, down = {"e4m3": (ml_dtypes.float8_e4m3fn, 7), "e5m2": (ml_dtypes.float8_e5m2, 14)}[fmt]
    v = np.moveaxis(np.asarray(x, np.float32).astype(ml_dtypes.bfloat16).astype(np.float64), axis, -1)
    blocks = v.reshape(v.shape[:-1] + (-1, 32))
    amax = np.abs(blocks).max(-1, keepdims=True)
    byte = np.maximum(np.where(amax > 0, np.frexp(amax)[1] - 1 + 127, 0) - down, 1)
    scale = np.exp2(byte - 127.0)
    codes = (blocks / scale).astype(np.float32).astype(dtype).astype(np.float64)
    return np.moveaxis((codes * scale).reshape(v.shape), -1, axis)


WIDE = False


def mx_kscale(k):
    if not WIDE:
        return np.ones(k)
    levels = np.array([10, -10, 5, -5, 0])
    a = np.random.permutation(np.resize(levels, k // 512 * 4)).reshape(k // 512, 4)
    idx = np.arange(k)
    return np.exp2(a[idx // 512, idx % 128 // 32])


BF16 = ml_dtypes.bfloat16


def bf(x):
    return np.asarray(x, np.float32).astype(BF16)


def f64(x):
    return np.asarray(x).astype(np.float64)


E2M1 = np.array([0.0, 0.5, 1.0, 1.5, 2.0, 3.0, 4.0, 6.0, -0.0, -0.5, -1.0, -1.5, -2.0, -3.0, -4.0, -6.0])


def pack_weight(w, fmt):
    k, n = w.shape
    w = f64(bf(w)).reshape(k // 32, 32, n)
    amax = np.abs(w).max(1)
    if fmt == "e4m3":
        byte = np.frexp(amax)[1] - 1 + 127 - 7
    else:
        mant, ex = np.frexp(amax / 6.0)
        byte = np.where(mant > 0.5, ex, ex - 1) + 127
    byte = np.clip(np.where(amax > 0, byte, 1), 1, 254)
    scaled = (w * np.exp2(127.0 - byte)[:, None, :]).reshape(k, n).astype(np.float32)
    by_word = np.ascontiguousarray(scaled.reshape(k // 512, 128, 4, n).transpose(0, 1, 3, 2))
    if fmt == "e4m3":
        words = by_word.astype(ml_dtypes.float8_e4m3fn).view(np.uint8)
    else:
        c = by_word.astype(ml_dtypes.float4_e2m1fn).view(np.uint8) & 0xF
        words = c[..., 0::2] | (c[..., 1::2] << 4)
    return np.ascontiguousarray(words), np.ascontiguousarray(byte.astype(np.uint8).reshape(k // 512, 16, n))


def unpack_weight(words, scales, fmt):
    g, p, n, _ = words.shape
    if fmt == "e4m3":
        vals = np.ascontiguousarray(words).view(ml_dtypes.float8_e4m3fn).astype(np.float64)
    else:
        nib = np.empty((g, p, n, 4), np.uint8)
        nib[..., 0::2] = words & 0xF
        nib[..., 1::2] = words >> 4
        vals = E2M1[nib]
    vals = vals * np.repeat(np.exp2(scales.astype(np.float64) - 127.0), 8, axis=1)[..., None]
    return vals.transpose(0, 1, 3, 2).reshape(g * 512, n)

def pack4(w):
    words, scales = pack_weight(w, "e2m1")
    return words.reshape(words.shape[0], 128, -1), scales


def unpack4(words, scales):
    return unpack_weight(words.reshape(words.shape[0], 128, -1, 2), scales, "e2m1")


B, N, C0, C1, C2, O0, O1, O2 = 16, 32, 512, 256, 256, 512, 2048, 256
G = C1 + C2
K = 2 * G


def sigmoid(v):
    return 1.0 / (1.0 + np.exp(-v))


def setup_inputs():
    s = mx_kscale(G)
    ss = np.concatenate([s, s])
    x1 = bf(np.random.random((B, N, C1)) * s[:C1])
    x2 = bf(np.random.random((B, N, N, C2)) * s[C1:])
    W2_words, W2_scales = pack4(np.random.standard_normal((K, O2)) * 2.0 / np.sqrt(K) / ss[:, None])
    b2 = bf(np.random.standard_normal(O2) * 0.3)
    return {"x1": x1,
            "x2": x2,
            "W2_words": W2_words,
            "W2_scales": W2_scales,
            "b2": b2}


def reference(x1, x2, W2_words, W2_scales, b2):
    x1, x2 = f64(x1), f64(x2)
    e1 = np.broadcast_to(x1[:, :, None, :], (B, N, N, C1))
    g = np.concatenate([e1, x2], axis=-1)
    f2 = np.concatenate([g, np.swapaxes(g, 1, 2)], axis=-1)
    return sigmoid((mxq(f2, 3, "e4m3") @ unpack4(W2_words, W2_scales)) + f64(b2))

@@ -1,0 +1,218 @@
+import concourse.mybir as mybir
+from concourse.masks import make_identity
+
+F32 = mybir.dt.float32
+BF16 = mybir.dt.bfloat16
+I32 = mybir.dt.int32
+U32 = mybir.dt.uint32
+U8 = mybir.dt.uint8
+FP8X4 = mybir.dt.float8_e4m3fn_x4
+FP4X4 = mybir.dt.float4_e2m1fn_x4
+ADD = mybir.AluOpType.add
+SIGMOID = mybir.ActivationFunctionType.Sigmoid
+
+P = 128
+SCENES = 16
+OBJECTS = 32
+CH = 256
+HALF = 64
+BLOCK = 8
+BLOCKS = OBJECTS // BLOCK
+WORDS = CH // 2
+TILES_PER_BANK = 2
+TILES_PER_STEP = 4
+
+FLOPS = 2 * SCENES * OBJECTS * OBJECTS * 4 * CH * CH
+
+
+def load_weight_quarter(nc, words, plane, W2_words, W2_scales, group, source_half, half, side):
+    nc.sync.dma_start(
+        out=words[HALF * half : HALF * (half + 1), 2 * CH * side : 2 * CH * (side + 1)].bitcast(I32),
+        in_=W2_words[group, HALF * source_half : HALF * (source_half + 1), :].bitcast(I32),
+    )
+    for quad in range(2):
+        first = HALF * half + 32 * quad
+        row = 8 * source_half + 4 * quad
+        nc.sync.dma_start(
+            out=plane[first : first + 4, CH * side : CH * (side + 1)].bitcast(I32),
+            in_=W2_scales[group, row : row + 4, :].bitcast(I32),
+        )
+
+
+def transpose_row_pairs(nc, bank, row_pairs, identity):
+    for t in range(TILES_PER_BANK):
+        for u in range(2):
+            nc.tensor.transpose(bank[:, t, u, :], row_pairs[t][:, u : 2 * WORDS : 2], identity[:])
+
+
+def tile_differentiablelogicmachine_pa_t_kernel(tc, x1, x2, W2_words, W2_scales, b2, out):
+    nc = tc.nc
+    block_pairs = [(p, q) for p in range(BLOCKS) for q in range(p, BLOCKS)]
+
+    with tc.tile_pool(name="const", bufs=1) as const, tc.tile_pool(
+        name="rows", bufs=len(block_pairs)
+    ) as rows_pool, tc.tile_pool(name="quant", bufs=2) as quant_pool, tc.tile_pool(
+        name="result", bufs=4
+    ) as result_pool, tc.psum_pool(name="flip", bufs=4) as flip_pool, tc.psum_pool(
+        name="acc", bufs=4
+    ) as acc_pool:
+        w_x2 = const.tile([P, 4 * CH], U8, align_bytes=64)
+        s_x2 = const.tile([P, 2 * CH], U8, align_bytes=64)
+        w_x1 = [const.tile([P, 4 * CH], U8, name="w_x1_%d" % h, align_bytes=64) for h in range(2)]
+        s_x1 = [const.tile([P, 2 * CH], U8, name="s_x1_%d" % h, align_bytes=64) for h in range(2)]
+        nc.vector.memset(s_x2[:].bitcast(I32), 0)
+        for h in range(2):
+            nc.vector.memset(w_x1[h][:].bitcast(I32), 0)
+            nc.vector.memset(s_x1[h][:].bitcast(I32), 0)
+        for h in range(2):
+            load_weight_quarter(nc, w_x1[h], s_x1[h], W2_words, W2_scales, 1, 0, h, 0)
+            load_weight_quarter(nc, w_x1[h], s_x1[h], W2_words, W2_scales, 0, 0, h, 1)
+        load_weight_quarter(nc, w_x2, s_x2, W2_words, W2_scales, 0, 1, 0, 0)
+        load_weight_quarter(nc, w_x2, s_x2, W2_words, W2_scales, 1, 1, 1, 0)
+        load_weight_quarter(nc, w_x2, s_x2, W2_words, W2_scales, 1, 1, 0, 1)
+        load_weight_quarter(nc, w_x2, s_x2, W2_words, W2_scales, 0, 1, 1, 1)
+
+        x1_rows = const.tile([P, BLOCKS, CH], BF16)
+        for p in range(BLOCKS):
+            nc.scalar.dma_start(out=x1_rows[:, p, :], in_=x1[:, BLOCK * p : BLOCK * (p + 1), :])
+        b2_bf = const.tile([P, CH], BF16)
+        nc.scalar.dma_start(out=b2_bf[:], in_=b2.partition_broadcast(P))
+
+        x2_rows = []
+        for p, q in block_pairs:
+            rows = rows_pool.tile([P, BLOCK, 2, CH], BF16)
+            for d in range(BLOCK):
+                i0, j = BLOCK * p, BLOCK * q + d
+                nc.sync.dma_start(out=rows[:, d, 0, :], in_=x2[:, i0 : i0 + BLOCK, j, :])
+                nc.sync.dma_start(out=rows[:, d, 1, :], in_=x2[:, j, i0 : i0 + BLOCK, :])
+            x2_rows.append(rows)
+
+        identity = const.tile([P, P], F32)
+        make_identity(nc, identity[:])
+        b2_f32 = const.tile([P, CH], F32)
+        nc.vector.tensor_copy(out=b2_f32[:], in_=b2_bf[:])
+
+        x1_bank = flip_pool.tile([P, TILES_PER_BANK, 2, P], F32, tag="bank")
+        transpose_row_pairs(
+            nc,
+            x1_bank,
+            [x1_rows[:, 2 * s : 2 * s + 2, :].rearrange("c h k -> c (h k)").bitcast(F32) for s in range(2)],
+            identity,
+        )
+        x1_grouped = const.tile([P, 2, P, 4], BF16, align_bytes=64)
+        nc.vector.tensor_copy(out=x1_grouped[:].bitcast(F32), in_=x1_bank[:].rearrange("n s u c -> n s c u"))
+        x1_codes = const.tile([P, 2, P], U32, align_bytes=64)
+        x1_plane = const.tile([P, 2, P], U8, align_bytes=64)
+        rep_grouped = const.tile([P, 2 * BLOCK, P, 4], BF16, align_bytes=64)
+        rep_codes = const.tile([P, 2 * BLOCK, P], U32, align_bytes=64)
+        rep_plane = const.tile([P, 2 * BLOCK, P], U8, align_bytes=64)
+        for s in range(2):
+            for d in range(BLOCK):
+                one = x1_grouped[:, s, :, :].bitcast(F32).rearrange("n (b a) u -> n b a u", a=BLOCK)
+                nc.vector.tensor_copy(
+                    out=rep_grouped[:, BLOCK * s + d, :, :].bitcast(F32).rearrange("n (b r) u -> n b r u", r=BLOCK),
+                    in_=one[:, :, d : d + 1, :].to_broadcast([P, SCENES, BLOCK, 2]),
+                )
+        nc.vector.quantize_mx(
+            out=x1_codes[:].rearrange("n s c -> n (s c)").bitcast(FP8X4),
+            scales=x1_plane[:].rearrange("n s c -> n (s c)"),
+            in_=x1_grouped[:].rearrange("n s c t -> n (s c t)"),
+        )
+        for s in range(2):
+            tiles = slice(BLOCK * s, BLOCK * (s + 1))
+            nc.vector.quantize_mx(
+                out=rep_codes[:, tiles, :].rearrange("n d c -> n (d c)").bitcast(FP8X4),
+                scales=rep_plane[:, tiles, :].rearrange("n d c -> n (d c)"),
+                in_=rep_grouped[:, tiles, :, :].rearrange("n d c t -> n (d c t)"),
+            )
+
+        own = const.tile([P, BLOCKS, 2 * CH], F32)
+        for p in range(BLOCKS):
+            vu = acc_pool.tile([P, 2 * CH], F32, tag="acc")
+            nc.tensor.matmul_mx(
+                out=vu[:],
+                lhsT=x1_codes[:, p // 2, :].bitcast(FP8X4),
+                lhsT_scale=x1_plane[:, p // 2, :],
+                rhs=w_x1[p % 2][:].bitcast(FP4X4),
+                rhs_scale=s_x1[p % 2][:],
+                start=True,
+                stop=True,
+            )
+            nc.vector.tensor_tensor(out=own[:, p, 0:CH], in0=vu[:, CH : 2 * CH], in1=b2_f32[:], op=ADD)
+            nc.vector.tensor_tensor(out=own[:, p, CH : 2 * CH], in0=vu[:, 0:CH], in1=b2_f32[:], op=ADD)
+
+        def quantise_block_pair(rows):
+            grouped = quant_pool.tile([P, BLOCK, P, 4], BF16, align_bytes=64)
+            codes = quant_pool.tile([P, BLOCK, P], U32, align_bytes=64)
+            plane = quant_pool.tile([P, BLOCK, P], U8, align_bytes=64)
+            for d0 in range(0, BLOCK, TILES_PER_BANK):
+                bank = flip_pool.tile([P, TILES_PER_BANK, 2, P], F32, tag="bank")
+                transpose_row_pairs(
+                    nc,
+                    bank,
+                    [rows[:, d0 + t, :, :].rearrange("c h k -> c (h k)").bitcast(F32) for t in range(TILES_PER_BANK)],
+                    identity,
+                )
+                nc.scalar.copy(
+                    out=grouped[:, d0 : d0 + TILES_PER_BANK, :, :].bitcast(F32),
+                    in_=bank[:].rearrange("n t u c -> n t c u"),
+                )
+            for d0 in range(0, BLOCK, TILES_PER_STEP):
+                tiles = slice(d0, d0 + TILES_PER_STEP)
+                nc.vector.quantize_mx(
+                    out=codes[:, tiles, :].rearrange("n d c -> n (d c)").bitcast(FP8X4),
+                    scales=plane[:, tiles, :].rearrange("n d c -> n (d c)"),
+                    in_=grouped[:, tiles, :, :].rearrange("n d c t -> n (d c t)"),
+                )
+            return codes, plane
+
+        def finish_block_pair(p, q, codes, plane):
+            both = q > p
+            sides = 2 if both else 1
+            width = 2 * CH if both else CH // 2
+            result = result_pool.tile([P, 2, BLOCK, CH], F32)
+            i0, j0 = BLOCK * p, BLOCK * q
+            for d in range(BLOCK):
+                acc = acc_pool.tile([P, 2 * CH], F32, tag="acc")
+                for c0 in range(0, sides * CH, width):
+                    nc.tensor.matmul_mx(
+                        out=acc[:, c0 : c0 + width],
+                        lhsT=codes[:, d, :].bitcast(FP8X4),
+                        lhsT_scale=plane[:, d, :],
+                        rhs=w_x2[:, 2 * c0 : 2 * (c0 + width)].bitcast(FP4X4),
+                        rhs_scale=s_x2[:, c0 : c0 + width],
+                        start=True,
+                        stop=False,
+                    )
+                    nc.tensor.matmul_mx(
+                        out=acc[:, c0 : c0 + width],
+                        lhsT=rep_codes[:, BLOCK * (q // 2) + d, :].bitcast(FP8X4),
+                        lhsT_scale=rep_plane[:, BLOCK * (q // 2) + d, :],
+                        rhs=w_x1[q % 2][:, 2 * c0 : 2 * (c0 + width)].bitcast(FP4X4),
+                        rhs_scale=s_x1[q % 2][:, c0 : c0 + width],
+                        start=False,
+                        stop=True,
+                    )
+                nc.vector.tensor_tensor(
+                    out=result[:, 0:sides, d, :],
+                    in0=acc[:, 0 : sides * CH].rearrange("c (s o) -> c s o", s=sides),
+                    in1=own[:, p, 0 : sides * CH].rearrange("c (s o) -> c s o", s=sides),
+                    op=ADD,
+                )
+                if d % TILES_PER_STEP == TILES_PER_STEP - 1:
+                    d0 = d + 1 - TILES_PER_STEP
+                    done = result[:, 0:sides, d0 : d + 1, :]
+                    nc.scalar.activation(out=done, in_=done, func=SIGMOID)
+                    nc.sync.dma_start(
+                        out=out[:, i0 : i0 + BLOCK, j0 + d0 : j0 + d + 1, :].rearrange("b a j o -> b a (j o)"),
+                        in_=result[:, 0, d0 : d + 1, :].rearrange("c j o -> c (j o)"),
+                    )
+                    if both:
+                        for e in range(d0, d + 1):
+                            nc.sync.dma_start(out=out[:, j0 + e, i0 : i0 + BLOCK, :], in_=result[:, 1, e, :])
+
+        ready = quantise_block_pair(x2_rows[0])
+        for n, (p, q) in enumerate(block_pairs):
+            following = quantise_block_pair(x2_rows[n + 1]) if n + 1 < len(block_pairs) else None
+            finish_block_pair(p, q, ready[0], ready[1])
+            ready = following

@@ -21,6 +21,7 @@ BLOCKS = OBJECTS // BLOCK
 WORDS = CH // 2
 TILES_PER_BANK = 2
 TILES_PER_STEP = 4
+LOADS_AHEAD = 5
 
 FLOPS = 2 * SCENES * OBJECTS * OBJECTS * 4 * CH * CH
 
@@ -47,104 +48,33 @@ def transpose_row_pairs(nc, bank, row_pairs, identity):
 
 def tile_differentiablelogicmachine_pa_t_kernel(tc, x1, x2, W2_words, W2_scales, b2, out):
     nc = tc.nc
-    block_pairs = [(p, q) for p in range(BLOCKS) for q in range(p, BLOCKS)]
+    block_pairs = [(p, q) for p in range(BLOCKS) for q in range(p + 1, BLOCKS)]
+    block_pairs += [(p, p) for p in range(BLOCKS)]
+    count = len(block_pairs)
 
-    with tc.tile_pool(name="const", bufs=1) as const, tc.tile_pool(
-        name="rows", bufs=len(block_pairs)
-    ) as rows_pool, tc.tile_pool(name="quant", bufs=2) as quant_pool, tc.tile_pool(
-        name="result", bufs=4
-    ) as result_pool, tc.psum_pool(name="flip", bufs=4) as flip_pool, tc.psum_pool(
-        name="acc", bufs=4
-    ) as acc_pool:
-        w_x2 = const.tile([P, 4 * CH], U8, align_bytes=64)
-        s_x2 = const.tile([P, 2 * CH], U8, align_bytes=64)
-        w_x1 = [const.tile([P, 4 * CH], U8, name="w_x1_%d" % h, align_bytes=64) for h in range(2)]
-        s_x1 = [const.tile([P, 2 * CH], U8, name="s_x1_%d" % h, align_bytes=64) for h in range(2)]
-        nc.vector.memset(s_x2[:].bitcast(I32), 0)
-        for h in range(2):
-            nc.vector.memset(w_x1[h][:].bitcast(I32), 0)
-            nc.vector.memset(s_x1[h][:].bitcast(I32), 0)
-        for h in range(2):
-            load_weight_quarter(nc, w_x1[h], s_x1[h], W2_words, W2_scales, 1, 0, h, 0)
-            load_weight_quarter(nc, w_x1[h], s_x1[h], W2_words, W2_scales, 0, 0, h, 1)
-        load_weight_quarter(nc, w_x2, s_x2, W2_words, W2_scales, 0, 1, 0, 0)
-        load_weight_quarter(nc, w_x2, s_x2, W2_words, W2_scales, 1, 1, 1, 0)
-        load_weight_quarter(nc, w_x2, s_x2, W2_words, W2_scales, 1, 1, 0, 1)
-        load_weight_quarter(nc, w_x2, s_x2, W2_words, W2_scales, 0, 1, 1, 1)
+    with tc.tile_pool(name="const", bufs=1) as const, tc.tile_pool(name="rows", bufs=count) as rows_pool, tc.tile_pool(
+        name="quant", bufs=2
+    ) as quant_pool, tc.tile_pool(name="result", bufs=4) as result_pool, tc.psum_pool(
+        name="flip", bufs=4
+    ) as flip_pool, tc.psum_pool(name="acc", bufs=4) as acc_pool, tc.manual_schedule():
+        x2_rows = {}
+        x2_grouped = {}
+        x2_codes = {}
+        x2_plane = {}
+        results = {}
 
-        x1_rows = const.tile([P, BLOCKS, CH], BF16)
-        for p in range(BLOCKS):
-            nc.scalar.dma_start(out=x1_rows[:, p, :], in_=x1[:, BLOCK * p : BLOCK * (p + 1), :])
-        b2_bf = const.tile([P, CH], BF16)
-        nc.scalar.dma_start(out=b2_bf[:], in_=b2.partition_broadcast(P))
-
-        x2_rows = []
-        for p, q in block_pairs:
+        def load_block_pair(n):
+            p, q = block_pairs[n]
             rows = rows_pool.tile([P, BLOCK, 2, CH], BF16)
             for d in range(BLOCK):
                 i0, j = BLOCK * p, BLOCK * q + d
                 nc.sync.dma_start(out=rows[:, d, 0, :], in_=x2[:, i0 : i0 + BLOCK, j, :])
                 nc.sync.dma_start(out=rows[:, d, 1, :], in_=x2[:, j, i0 : i0 + BLOCK, :])
-            x2_rows.append(rows)
+            x2_rows[n] = rows
 
-        identity = const.tile([P, P], F32)
-        make_identity(nc, identity[:])
-        b2_f32 = const.tile([P, CH], F32)
-        nc.vector.tensor_copy(out=b2_f32[:], in_=b2_bf[:])
-
-        x1_bank = flip_pool.tile([P, TILES_PER_BANK, 2, P], F32, tag="bank")
-        transpose_row_pairs(
-            nc,
-            x1_bank,
-            [x1_rows[:, 2 * s : 2 * s + 2, :].rearrange("c h k -> c (h k)").bitcast(F32) for s in range(2)],
-            identity,
-        )
-        x1_grouped = const.tile([P, 2, P, 4], BF16, align_bytes=64)
-        nc.vector.tensor_copy(out=x1_grouped[:].bitcast(F32), in_=x1_bank[:].rearrange("n s u c -> n s c u"))
-        x1_codes = const.tile([P, 2, P], U32, align_bytes=64)
-        x1_plane = const.tile([P, 2, P], U8, align_bytes=64)
-        rep_grouped = const.tile([P, 2 * BLOCK, P, 4], BF16, align_bytes=64)
-        rep_codes = const.tile([P, 2 * BLOCK, P], U32, align_bytes=64)
-        rep_plane = const.tile([P, 2 * BLOCK, P], U8, align_bytes=64)
-        for s in range(2):
-            for d in range(BLOCK):
-                one = x1_grouped[:, s, :, :].bitcast(F32).rearrange("n (b a) u -> n b a u", a=BLOCK)
-                nc.vector.tensor_copy(
-                    out=rep_grouped[:, BLOCK * s + d, :, :].bitcast(F32).rearrange("n (b r) u -> n b r u", r=BLOCK),
-                    in_=one[:, :, d : d + 1, :].to_broadcast([P, SCENES, BLOCK, 2]),
-                )
-        nc.vector.quantize_mx(
-            out=x1_codes[:].rearrange("n s c -> n (s c)").bitcast(FP8X4),
-            scales=x1_plane[:].rearrange("n s c -> n (s c)"),
-            in_=x1_grouped[:].rearrange("n s c t -> n (s c t)"),
-        )
-        for s in range(2):
-            tiles = slice(BLOCK * s, BLOCK * (s + 1))
-            nc.vector.quantize_mx(
-                out=rep_codes[:, tiles, :].rearrange("n d c -> n (d c)").bitcast(FP8X4),
-                scales=rep_plane[:, tiles, :].rearrange("n d c -> n (d c)"),
-                in_=rep_grouped[:, tiles, :, :].rearrange("n d c t -> n (d c t)"),
-            )
-
-        own = const.tile([P, BLOCKS, 2 * CH], F32)
-        for p in range(BLOCKS):
-            vu = acc_pool.tile([P, 2 * CH], F32, tag="acc")
-            nc.tensor.matmul_mx(
-                out=vu[:],
-                lhsT=x1_codes[:, p // 2, :].bitcast(FP8X4),
-                lhsT_scale=x1_plane[:, p // 2, :],
-                rhs=w_x1[p % 2][:].bitcast(FP4X4),
-                rhs_scale=s_x1[p % 2][:],
-                start=True,
-                stop=True,
-            )
-            nc.vector.tensor_tensor(out=own[:, p, 0:CH], in0=vu[:, CH : 2 * CH], in1=b2_f32[:], op=ADD)
-            nc.vector.tensor_tensor(out=own[:, p, CH : 2 * CH], in0=vu[:, 0:CH], in1=b2_f32[:], op=ADD)
-
-        def quantise_block_pair(rows):
+        def flip_block_pair(n):
+            rows = x2_rows[n]
             grouped = quant_pool.tile([P, BLOCK, P, 4], BF16, align_bytes=64)
-            codes = quant_pool.tile([P, BLOCK, P], U32, align_bytes=64)
-            plane = quant_pool.tile([P, BLOCK, P], U8, align_bytes=64)
             for d0 in range(0, BLOCK, TILES_PER_BANK):
                 bank = flip_pool.tile([P, TILES_PER_BANK, 2, P], F32, tag="bank")
                 transpose_row_pairs(
@@ -157,6 +87,12 @@ def tile_differentiablelogicmachine_pa_t_kernel(tc, x1, x2, W2_words, W2_scales,
                     out=grouped[:, d0 : d0 + TILES_PER_BANK, :, :].bitcast(F32),
                     in_=bank[:].rearrange("n t u c -> n t c u"),
                 )
+            x2_grouped[n] = grouped
+
+        def quantise_block_pair(n):
+            grouped = x2_grouped[n]
+            codes = quant_pool.tile([P, BLOCK, P], U32, align_bytes=64)
+            plane = quant_pool.tile([P, BLOCK, P], U8, align_bytes=64)
             for d0 in range(0, BLOCK, TILES_PER_STEP):
                 tiles = slice(d0, d0 + TILES_PER_STEP)
                 nc.vector.quantize_mx(
@@ -164,21 +100,23 @@ def tile_differentiablelogicmachine_pa_t_kernel(tc, x1, x2, W2_words, W2_scales,
                     scales=plane[:, tiles, :].rearrange("n d c -> n (d c)"),
                     in_=grouped[:, tiles, :, :].rearrange("n d c t -> n (d c t)"),
                 )
-            return codes, plane
+            x2_codes[n] = codes
+            x2_plane[n] = plane
 
-        def finish_block_pair(p, q, codes, plane):
-            both = q > p
-            sides = 2 if both else 1
-            width = 2 * CH if both else CH // 2
-            result = result_pool.tile([P, 2, BLOCK, CH], F32)
-            i0, j0 = BLOCK * p, BLOCK * q
-            for d in range(BLOCK):
+        def multiply_step(n, d0):
+            p, q = block_pairs[n]
+            sides = 2 if q > p else 1
+            width = 2 * CH if q > p else CH // 2
+            if d0 == 0:
+                result = result_pool.tile([P, 2, BLOCK, CH], F32)
+                results[n] = result
+            for d in range(d0, d0 + TILES_PER_STEP):
                 acc = acc_pool.tile([P, 2 * CH], F32, tag="acc")
                 for c0 in range(0, sides * CH, width):
                     nc.tensor.matmul_mx(
                         out=acc[:, c0 : c0 + width],
-                        lhsT=codes[:, d, :].bitcast(FP8X4),
-                        lhsT_scale=plane[:, d, :],
+                        lhsT=x2_codes[n][:, d, :].bitcast(FP8X4),
+                        lhsT_scale=x2_plane[n][:, d, :],
                         rhs=w_x2[:, 2 * c0 : 2 * (c0 + width)].bitcast(FP4X4),
                         rhs_scale=s_x2[:, c0 : c0 + width],
                         start=True,
@@ -194,25 +132,123 @@ def tile_differentiablelogicmachine_pa_t_kernel(tc, x1, x2, W2_words, W2_scales,
                         stop=True,
                     )
                 nc.vector.tensor_tensor(
-                    out=result[:, 0:sides, d, :],
+                    out=results[n][:, 0:sides, d, :],
                     in0=acc[:, 0 : sides * CH].rearrange("c (s o) -> c s o", s=sides),
                     in1=own[:, p, 0 : sides * CH].rearrange("c (s o) -> c s o", s=sides),
                     op=ADD,
                 )
-                if d % TILES_PER_STEP == TILES_PER_STEP - 1:
-                    d0 = d + 1 - TILES_PER_STEP
-                    done = result[:, 0:sides, d0 : d + 1, :]
-                    nc.scalar.activation(out=done, in_=done, func=SIGMOID)
-                    nc.sync.dma_start(
-                        out=out[:, i0 : i0 + BLOCK, j0 + d0 : j0 + d + 1, :].rearrange("b a j o -> b a (j o)"),
-                        in_=result[:, 0, d0 : d + 1, :].rearrange("c j o -> c (j o)"),
-                    )
-                    if both:
-                        for e in range(d0, d + 1):
-                            nc.sync.dma_start(out=out[:, j0 + e, i0 : i0 + BLOCK, :], in_=result[:, 1, e, :])
 
-        ready = quantise_block_pair(x2_rows[0])
-        for n, (p, q) in enumerate(block_pairs):
-            following = quantise_block_pair(x2_rows[n + 1]) if n + 1 < len(block_pairs) else None
-            finish_block_pair(p, q, ready[0], ready[1])
-            ready = following
+        def finish_step(n, d0):
+            p, q = block_pairs[n]
+            sides = 2 if q > p else 1
+            i0, j0 = BLOCK * p, BLOCK * q
+            d1 = d0 + TILES_PER_STEP
+            done = results[n][:, 0:sides, d0:d1, :]
+            nc.scalar.activation(out=done, in_=done, func=SIGMOID)
+            nc.sync.dma_start(
+                out=out[:, i0 : i0 + BLOCK, j0 + d0 : j0 + d1, :].rearrange("b a j o -> b a (j o)"),
+                in_=results[n][:, 0, d0:d1, :].rearrange("c j o -> c (j o)"),
+            )
+            if q > p:
+                for d in range(d0, d1):
+                    nc.sync.dma_start(out=out[:, j0 + d, i0 : i0 + BLOCK, :], in_=results[n][:, 1, d, :])
+
+        x1_rows = const.tile([P, BLOCKS, CH], BF16)
+        for p in range(BLOCKS):
+            nc.sync.dma_start(out=x1_rows[:, p, :], in_=x1[:, BLOCK * p : BLOCK * (p + 1), :])
+        load_block_pair(0)
+
+        w_x2 = const.tile([P, 4 * CH], U8, align_bytes=64)
+        s_x2 = const.tile([P, 2 * CH], U8, align_bytes=64)
+        w_x1 = [const.tile([P, 4 * CH], U8, name="w_x1_%d" % h, align_bytes=64) for h in range(2)]
+        s_x1 = [const.tile([P, 2 * CH], U8, name="s_x1_%d" % h, align_bytes=64) for h in range(2)]
+        for h in range(2):
+            nc.vector.memset(w_x1[h][:].bitcast(I32), 0)
+            nc.vector.memset(s_x1[h][:].bitcast(I32), 0)
+        nc.vector.memset(s_x2[:].bitcast(I32), 0)
+        for h in range(2):
+            load_weight_quarter(nc, w_x1[h], s_x1[h], W2_words, W2_scales, 1, 0, h, 0)
+            load_weight_quarter(nc, w_x1[h], s_x1[h], W2_words, W2_scales, 0, 0, h, 1)
+        b2_bf = const.tile([P, CH], BF16)
+        nc.sync.dma_start(out=b2_bf[:], in_=b2.partition_broadcast(P))
+        load_weight_quarter(nc, w_x2, s_x2, W2_words, W2_scales, 0, 1, 0, 0)
+        load_weight_quarter(nc, w_x2, s_x2, W2_words, W2_scales, 1, 1, 1, 0)
+        load_weight_quarter(nc, w_x2, s_x2, W2_words, W2_scales, 1, 1, 0, 1)
+        load_weight_quarter(nc, w_x2, s_x2, W2_words, W2_scales, 0, 1, 1, 1)
+        for n in range(1, LOADS_AHEAD):
+            load_block_pair(n)
+
+        identity = const.tile([P, P], F32)
+        make_identity(nc, identity[:])
+        warm = const.tile([P, 1], F32)
+        nc.vector.memset(warm[:], 0.0)
+        nc.scalar.activation(out=warm[:], in_=warm[:], func=SIGMOID)
+
+        x1_bank = flip_pool.tile([P, TILES_PER_BANK, 2, P], F32, tag="bank")
+        transpose_row_pairs(
+            nc,
+            x1_bank,
+            [x1_rows[:, 2 * s : 2 * s + 2, :].rearrange("c h k -> c (h k)").bitcast(F32) for s in range(2)],
+            identity,
+        )
+        flip_block_pair(0)
+        flip_block_pair(1)
+        x1_grouped = const.tile([P, 2, P, 4], BF16, align_bytes=64)
+        nc.vector.tensor_copy(out=x1_grouped[:].bitcast(F32), in_=x1_bank[:].rearrange("n s u c -> n s c u"))
+        x1_codes = const.tile([P, 2, P], U32, align_bytes=64)
+        x1_plane = const.tile([P, 2, P], U8, align_bytes=64)
+        rep_grouped = const.tile([P, 2 * BLOCK, P, 4], BF16, align_bytes=64)
+        rep_codes = const.tile([P, 2 * BLOCK, P], U32, align_bytes=64)
+        rep_plane = const.tile([P, 2 * BLOCK, P], U8, align_bytes=64)
+        b2_f32 = const.tile([P, CH], F32)
+        own = const.tile([P, BLOCKS, 2 * CH], F32)
+        for s in range(2):
+            for d in range(BLOCK):
+                one = x1_grouped[:, s, :, :].bitcast(F32).rearrange("n (b a) u -> n b a u", a=BLOCK)
+                nc.vector.tensor_copy(
+                    out=rep_grouped[:, BLOCK * s + d, :, :].bitcast(F32).rearrange("n (b r) u -> n b r u", r=BLOCK),
+                    in_=one[:, :, d : d + 1, :].to_broadcast([P, SCENES, BLOCK, 2]),
+                )
+            if s == 0:
+                nc.vector.quantize_mx(
+                    out=x1_codes[:].rearrange("n s c -> n (s c)").bitcast(FP8X4),
+                    scales=x1_plane[:].rearrange("n s c -> n (s c)"),
+                    in_=x1_grouped[:].rearrange("n s c t -> n (s c t)"),
+                )
+            tiles = slice(BLOCK * s, BLOCK * (s + 1))
+            nc.vector.quantize_mx(
+                out=rep_codes[:, tiles, :].rearrange("n d c -> n (d c)").bitcast(FP8X4),
+                scales=rep_plane[:, tiles, :].rearrange("n d c -> n (d c)"),
+                in_=rep_grouped[:, tiles, :, :].rearrange("n d c t -> n (d c t)"),
+            )
+            if s == 0:
+                quantise_block_pair(0)
+                nc.vector.tensor_copy(out=b2_f32[:], in_=b2_bf[:])
+                for p in range(BLOCKS):
+                    vu = acc_pool.tile([P, 2 * CH], F32, tag="acc")
+                    nc.tensor.matmul_mx(
+                        out=vu[:],
+                        lhsT=x1_codes[:, p // 2, :].bitcast(FP8X4),
+                        lhsT_scale=x1_plane[:, p // 2, :],
+                        rhs=w_x1[p % 2][:].bitcast(FP4X4),
+                        rhs_scale=s_x1[p % 2][:],
+                        start=True,
+                        stop=True,
+                    )
+                    nc.vector.tensor_tensor(out=own[:, p, 0:CH], in0=vu[:, CH : 2 * CH], in1=b2_f32[:], op=ADD)
+                    nc.vector.tensor_tensor(out=own[:, p, CH : 2 * CH], in0=vu[:, 0:CH], in1=b2_f32[:], op=ADD)
+
+        waiting = None
+        for n in range(count):
+            if n + LOADS_AHEAD < count:
+                load_block_pair(n + LOADS_AHEAD)
+            if n + 2 < count:
+                flip_block_pair(n + 2)
+            if n + 1 < count:
+                quantise_block_pair(n + 1)
+            for d0 in range(0, BLOCK, TILES_PER_STEP):
+                multiply_step(n, d0)
+                if waiting is not None:
+                    finish_step(waiting[0], waiting[1])
+                waiting = (n, d0)
+        finish_step(waiting[0], waiting[1])

@@ -21,7 +21,6 @@ BLOCKS = OBJECTS // BLOCK
 WORDS = CH // 2
 TILES_PER_BANK = 2
 TILES_PER_STEP = 4
-LOADS_AHEAD = 5
 
 FLOPS = 2 * SCENES * OBJECTS * OBJECTS * 4 * CH * CH
 
@@ -145,13 +144,14 @@ def tile_differentiablelogicmachine_pa_t_kernel(tc, x1, x2, W2_words, W2_scales,
             d1 = d0 + TILES_PER_STEP
             done = results[n][:, 0:sides, d0:d1, :]
             nc.scalar.activation(out=done, in_=done, func=SIGMOID)
-            nc.sync.dma_start(
-                out=out[:, i0 : i0 + BLOCK, j0 + d0 : j0 + d1, :].rearrange("b a j o -> b a (j o)"),
-                in_=results[n][:, 0, d0:d1, :].rearrange("c j o -> c (j o)"),
-            )
             if q > p:
                 for d in range(d0, d1):
-                    nc.sync.dma_start(out=out[:, j0 + d, i0 : i0 + BLOCK, :], in_=results[n][:, 1, d, :])
+                    nc.gpsimd.dma_start(out=out[:, j0 + d, i0 : i0 + BLOCK, :], in_=results[n][:, 1, d, :])
+            if d1 == BLOCK:
+                nc.gpsimd.dma_start(
+                    out=out[:, i0 : i0 + BLOCK, j0 : j0 + BLOCK, :].rearrange("b a j o -> b a (j o)"),
+                    in_=results[n][:, 0, :, :].rearrange("c j o -> c (j o)"),
+                )
 
         x1_rows = const.tile([P, BLOCKS, CH], BF16)
         for p in range(BLOCKS):
@@ -175,7 +175,7 @@ def tile_differentiablelogicmachine_pa_t_kernel(tc, x1, x2, W2_words, W2_scales,
         load_weight_quarter(nc, w_x2, s_x2, W2_words, W2_scales, 1, 1, 1, 0)
         load_weight_quarter(nc, w_x2, s_x2, W2_words, W2_scales, 1, 1, 0, 1)
         load_weight_quarter(nc, w_x2, s_x2, W2_words, W2_scales, 0, 1, 1, 1)
-        for n in range(1, LOADS_AHEAD):
+        for n in range(1, count):
             load_block_pair(n)
 
         identity = const.tile([P, P], F32)
@@ -240,8 +240,6 @@ def tile_differentiablelogicmachine_pa_t_kernel(tc, x1, x2, W2_words, W2_scales,
 
         waiting = None
         for n in range(count):
-            if n + LOADS_AHEAD < count:
-                load_block_pair(n + LOADS_AHEAD)
             if n + 2 < count:
                 flip_block_pair(n + 2)
             if n + 1 < count:

@@ -21,6 +21,7 @@ BLOCKS = OBJECTS // BLOCK
 WORDS = CH // 2
 TILES_PER_BANK = 2
 TILES_PER_STEP = 4
+LOADS_AHEAD = 5
 
 FLOPS = 2 * SCENES * OBJECTS * OBJECTS * 4 * CH * CH
 
@@ -144,14 +145,13 @@ def tile_differentiablelogicmachine_pa_t_kernel(tc, x1, x2, W2_words, W2_scales,
             d1 = d0 + TILES_PER_STEP
             done = results[n][:, 0:sides, d0:d1, :]
             nc.scalar.activation(out=done, in_=done, func=SIGMOID)
+            nc.gpsimd.dma_start(
+                out=out[:, i0 : i0 + BLOCK, j0 + d0 : j0 + d1, :].rearrange("b a j o -> b a (j o)"),
+                in_=results[n][:, 0, d0:d1, :].rearrange("c j o -> c (j o)"),
+            )
             if q > p:
                 for d in range(d0, d1):
-                    nc.gpsimd.dma_start(out=out[:, j0 + d, i0 : i0 + BLOCK, :], in_=results[n][:, 1, d, :])
-            if d1 == BLOCK:
-                nc.gpsimd.dma_start(
-                    out=out[:, i0 : i0 + BLOCK, j0 : j0 + BLOCK, :].rearrange("b a j o -> b a (j o)"),
-                    in_=results[n][:, 0, :, :].rearrange("c j o -> c (j o)"),
-                )
+                    nc.sync.dma_start(out=out[:, j0 + d, i0 : i0 + BLOCK, :], in_=results[n][:, 1, d, :])
 
         x1_rows = const.tile([P, BLOCKS, CH], BF16)
         for p in range(BLOCKS):
@@ -175,7 +175,7 @@ def tile_differentiablelogicmachine_pa_t_kernel(tc, x1, x2, W2_words, W2_scales,
         load_weight_quarter(nc, w_x2, s_x2, W2_words, W2_scales, 1, 1, 1, 0)
         load_weight_quarter(nc, w_x2, s_x2, W2_words, W2_scales, 1, 1, 0, 1)
         load_weight_quarter(nc, w_x2, s_x2, W2_words, W2_scales, 0, 1, 1, 1)
-        for n in range(1, count):
+        for n in range(1, LOADS_AHEAD):
             load_block_pair(n)
 
         identity = const.tile([P, P], F32)
@@ -240,6 +240,8 @@ def tile_differentiablelogicmachine_pa_t_kernel(tc, x1, x2, W2_words, W2_scales,
 
         waiting = None
         for n in range(count):
+            if n + LOADS_AHEAD < count:
+                load_block_pair(n + LOADS_AHEAD)
             if n + 2 < count:
                 flip_block_pair(n + 2)
             if n + 1 < count:

@@ -26,18 +26,31 @@ LOADS_AHEAD = 5
 FLOPS = 2 * SCENES * OBJECTS * OBJECTS * 4 * CH * CH
 
 
-def load_weight_quarter(nc, words, plane, W2_words, W2_scales, group, source_half, half, side):
-    nc.sync.dma_start(
-        out=words[HALF * half : HALF * (half + 1), 2 * CH * side : 2 * CH * (side + 1)].bitcast(I32),
-        in_=W2_words[group, HALF * source_half : HALF * (source_half + 1), :].bitcast(I32),
-    )
+def load_weight_half(nc, words, plane, W2_words, W2_scales, source_half, half, groups):
+    rows = slice(HALF * source_half, HALF * (source_half + 1))
+    to = slice(HALF * half, HALF * (half + 1))
+    if groups == (0, 1):
+        nc.sync.dma_start(out=words[to, :].bitcast(I32), in_=W2_words[:, rows, :].bitcast(I32).rearrange("g p n -> p g n"))
+    else:
+        for side in range(2):
+            nc.sync.dma_start(
+                out=words[to, 2 * CH * side : 2 * CH * (side + 1)].bitcast(I32),
+                in_=W2_words[groups[side], rows, :].bitcast(I32),
+            )
     for quad in range(2):
         first = HALF * half + 32 * quad
         row = 8 * source_half + 4 * quad
-        nc.sync.dma_start(
-            out=plane[first : first + 4, CH * side : CH * (side + 1)].bitcast(I32),
-            in_=W2_scales[group, row : row + 4, :].bitcast(I32),
-        )
+        if groups == (0, 1):
+            nc.sync.dma_start(
+                out=plane[first : first + 4, :].bitcast(I32),
+                in_=W2_scales[:, row : row + 4, :].bitcast(I32).rearrange("g r n -> r g n"),
+            )
+        else:
+            for side in range(2):
+                nc.sync.dma_start(
+                    out=plane[first : first + 4, CH * side : CH * (side + 1)].bitcast(I32),
+                    in_=W2_scales[groups[side], row : row + 4, :].bitcast(I32),
+                )
 
 
 def transpose_row_pairs(nc, bank, row_pairs, identity):
@@ -105,14 +118,14 @@ def tile_differentiablelogicmachine_pa_t_kernel(tc, x1, x2, W2_words, W2_scales,
 
         def multiply_step(n, d0):
             p, q = block_pairs[n]
-            sides = 2 if q > p else 1
+            first = 0 if q > p else 1
             width = 2 * CH if q > p else CH // 2
             if d0 == 0:
                 result = result_pool.tile([P, 2, BLOCK, CH], F32)
                 results[n] = result
             for d in range(d0, d0 + TILES_PER_STEP):
                 acc = acc_pool.tile([P, 2 * CH], F32, tag="acc")
-                for c0 in range(0, sides * CH, width):
+                for c0 in range(first * CH, 2 * CH, width):
                     nc.tensor.matmul_mx(
                         out=acc[:, c0 : c0 + width],
                         lhsT=x2_codes[n][:, d, :].bitcast(FP8X4),
@@ -132,31 +145,30 @@ def tile_differentiablelogicmachine_pa_t_kernel(tc, x1, x2, W2_words, W2_scales,
                         stop=True,
                     )
                 nc.vector.tensor_tensor(
-                    out=results[n][:, 0:sides, d, :],
-                    in0=acc[:, 0 : sides * CH].rearrange("c (s o) -> c s o", s=sides),
-                    in1=own[:, p, 0 : sides * CH].rearrange("c (s o) -> c s o", s=sides),
+                    out=results[n][:, first:2, d, :],
+                    in0=acc[:, first * CH : 2 * CH].rearrange("c (s o) -> c s o", o=CH),
+                    in1=own[:, p, first * CH : 2 * CH].rearrange("c (s o) -> c s o", o=CH),
                     op=ADD,
                 )
 
         def finish_step(n, d0):
             p, q = block_pairs[n]
-            sides = 2 if q > p else 1
+            first = 0 if q > p else 1
             i0, j0 = BLOCK * p, BLOCK * q
             d1 = d0 + TILES_PER_STEP
-            done = results[n][:, 0:sides, d0:d1, :]
+            done = results[n][:, first:2, d0:d1, :]
             nc.scalar.activation(out=done, in_=done, func=SIGMOID)
             nc.gpsimd.dma_start(
                 out=out[:, i0 : i0 + BLOCK, j0 + d0 : j0 + d1, :].rearrange("b a j o -> b a (j o)"),
-                in_=results[n][:, 0, d0:d1, :].rearrange("c j o -> c (j o)"),
+                in_=results[n][:, 1, d0:d1, :].rearrange("c j o -> c (j o)"),
             )
             if q > p:
                 for d in range(d0, d1):
-                    nc.sync.dma_start(out=out[:, j0 + d, i0 : i0 + BLOCK, :], in_=results[n][:, 1, d, :])
+                    nc.sync.dma_start(out=out[:, j0 + d, i0 : i0 + BLOCK, :], in_=results[n][:, 0, d, :])
 
         x1_rows = const.tile([P, BLOCKS, CH], BF16)
         for p in range(BLOCKS):
             nc.sync.dma_start(out=x1_rows[:, p, :], in_=x1[:, BLOCK * p : BLOCK * (p + 1), :])
-        load_block_pair(0)
 
         w_x2 = const.tile([P, 4 * CH], U8, align_bytes=64)
         s_x2 = const.tile([P, 2 * CH], U8, align_bytes=64)
@@ -166,15 +178,16 @@ def tile_differentiablelogicmachine_pa_t_kernel(tc, x1, x2, W2_words, W2_scales,
             nc.vector.memset(w_x1[h][:].bitcast(I32), 0)
             nc.vector.memset(s_x1[h][:].bitcast(I32), 0)
         nc.vector.memset(s_x2[:].bitcast(I32), 0)
+        b2_row = const.tile([P, CH], BF16)
+        nc.vector.memset(b2_row[:], 0.0)
+        ones = const.tile([P, P], BF16)
+        nc.vector.memset(ones[:], 1.0)
         for h in range(2):
-            load_weight_quarter(nc, w_x1[h], s_x1[h], W2_words, W2_scales, 1, 0, h, 0)
-            load_weight_quarter(nc, w_x1[h], s_x1[h], W2_words, W2_scales, 0, 0, h, 1)
-        b2_bf = const.tile([P, CH], BF16)
-        nc.sync.dma_start(out=b2_bf[:], in_=b2.partition_broadcast(P))
-        load_weight_quarter(nc, w_x2, s_x2, W2_words, W2_scales, 0, 1, 0, 0)
-        load_weight_quarter(nc, w_x2, s_x2, W2_words, W2_scales, 1, 1, 1, 0)
-        load_weight_quarter(nc, w_x2, s_x2, W2_words, W2_scales, 1, 1, 0, 1)
-        load_weight_quarter(nc, w_x2, s_x2, W2_words, W2_scales, 0, 1, 1, 1)
+            load_weight_half(nc, w_x1[h], s_x1[h], W2_words, W2_scales, 0, h, (0, 1))
+        nc.sync.dma_start(out=b2_row[0:1, :], in_=b2.rearrange("(x o) -> x o", x=1))
+        load_block_pair(0)
+        load_weight_half(nc, w_x2, s_x2, W2_words, W2_scales, 1, 0, (1, 0))
+        load_weight_half(nc, w_x2, s_x2, W2_words, W2_scales, 1, 1, (0, 1))
         for n in range(1, LOADS_AHEAD):
             load_block_pair(n)
 
@@ -191,8 +204,8 @@ def tile_differentiablelogicmachine_pa_t_kernel(tc, x1, x2, W2_words, W2_scales,
             [x1_rows[:, 2 * s : 2 * s + 2, :].rearrange("c h k -> c (h k)").bitcast(F32) for s in range(2)],
             identity,
         )
-        flip_block_pair(0)
-        flip_block_pair(1)
+        b2_bank = acc_pool.tile([P, 2 * CH], F32, tag="acc")
+        nc.tensor.matmul(b2_bank[:, 0:CH], lhsT=ones[:], rhs=b2_row[:], start=True, stop=True)
         x1_grouped = const.tile([P, 2, P, 4], BF16, align_bytes=64)
         nc.vector.tensor_copy(out=x1_grouped[:].bitcast(F32), in_=x1_bank[:].rearrange("n s u c -> n s c u"))
         x1_codes = const.tile([P, 2, P], U32, align_bytes=64)
@@ -202,41 +215,49 @@ def tile_differentiablelogicmachine_pa_t_kernel(tc, x1, x2, W2_words, W2_scales,
         rep_plane = const.tile([P, 2 * BLOCK, P], U8, align_bytes=64)
         b2_f32 = const.tile([P, CH], F32)
         own = const.tile([P, BLOCKS, 2 * CH], F32)
-        for s in range(2):
+        nc.vector.quantize_mx(
+            out=x1_codes[:].rearrange("n s c -> n (s c)").bitcast(FP8X4),
+            scales=x1_plane[:].rearrange("n s c -> n (s c)"),
+            in_=x1_grouped[:].rearrange("n s c t -> n (s c t)"),
+        )
+        nc.vector.tensor_copy(out=b2_f32[:], in_=b2_bank[:, 0:CH])
+
+        def repeat_rows(s):
+            one = x1_grouped[:, s, :, :].bitcast(F32).rearrange("n (b a) u -> n b a u", a=BLOCK)
             for d in range(BLOCK):
-                one = x1_grouped[:, s, :, :].bitcast(F32).rearrange("n (b a) u -> n b a u", a=BLOCK)
-                nc.vector.tensor_copy(
+                nc.scalar.copy(
                     out=rep_grouped[:, BLOCK * s + d, :, :].bitcast(F32).rearrange("n (b r) u -> n b r u", r=BLOCK),
                     in_=one[:, :, d : d + 1, :].to_broadcast([P, SCENES, BLOCK, 2]),
                 )
-            if s == 0:
-                nc.vector.quantize_mx(
-                    out=x1_codes[:].rearrange("n s c -> n (s c)").bitcast(FP8X4),
-                    scales=x1_plane[:].rearrange("n s c -> n (s c)"),
-                    in_=x1_grouped[:].rearrange("n s c t -> n (s c t)"),
-                )
+
+        def quantise_repeated(s):
             tiles = slice(BLOCK * s, BLOCK * (s + 1))
             nc.vector.quantize_mx(
                 out=rep_codes[:, tiles, :].rearrange("n d c -> n (d c)").bitcast(FP8X4),
                 scales=rep_plane[:, tiles, :].rearrange("n d c -> n (d c)"),
                 in_=rep_grouped[:, tiles, :, :].rearrange("n d c t -> n (d c t)"),
             )
-            if s == 0:
-                quantise_block_pair(0)
-                nc.vector.tensor_copy(out=b2_f32[:], in_=b2_bf[:])
-                for p in range(BLOCKS):
-                    vu = acc_pool.tile([P, 2 * CH], F32, tag="acc")
-                    nc.tensor.matmul_mx(
-                        out=vu[:],
-                        lhsT=x1_codes[:, p // 2, :].bitcast(FP8X4),
-                        lhsT_scale=x1_plane[:, p // 2, :],
-                        rhs=w_x1[p % 2][:].bitcast(FP4X4),
-                        rhs_scale=s_x1[p % 2][:],
-                        start=True,
-                        stop=True,
-                    )
-                    nc.vector.tensor_tensor(out=own[:, p, 0:CH], in0=vu[:, CH : 2 * CH], in1=b2_f32[:], op=ADD)
-                    nc.vector.tensor_tensor(out=own[:, p, CH : 2 * CH], in0=vu[:, 0:CH], in1=b2_f32[:], op=ADD)
+
+        def make_own(p):
+            uv = acc_pool.tile([P, 2 * CH], F32, tag="acc")
+            nc.tensor.matmul_mx(
+                out=uv[:],
+                lhsT=x1_codes[:, p // 2, :].bitcast(FP8X4),
+                lhsT_scale=x1_plane[:, p // 2, :],
+                rhs=w_x1[p % 2][:].bitcast(FP4X4),
+                rhs_scale=s_x1[p % 2][:],
+                start=True,
+                stop=True,
+            )
+            nc.vector.tensor_tensor(out=own[:, p, 0:CH], in0=uv[:, CH : 2 * CH], in1=b2_f32[:], op=ADD)
+            nc.vector.tensor_tensor(out=own[:, p, CH : 2 * CH], in0=uv[:, 0:CH], in1=b2_f32[:], op=ADD)
+
+        repeat_rows(0)
+        flip_block_pair(0)
+        make_own(0)
+        quantise_repeated(0)
+        quantise_block_pair(0)
+        flip_block_pair(1)
 
         waiting = None
         for n in range(count):
@@ -246,9 +267,15 @@ def tile_differentiablelogicmachine_pa_t_kernel(tc, x1, x2, W2_words, W2_scales,
                 flip_block_pair(n + 2)
             if n + 1 < count:
                 quantise_block_pair(n + 1)
+            if n == 0:
+                repeat_rows(1)
             for d0 in range(0, BLOCK, TILES_PER_STEP):
                 multiply_step(n, d0)
                 if waiting is not None:
                     finish_step(waiting[0], waiting[1])
                 waiting = (n, d0)
+            if n == 0:
+                quantise_repeated(1)
+            if n + 1 < BLOCKS:
+                make_own(n + 1)
         finish_step(waiting[0], waiting[1])

@@ -53,6 +53,20 @@ def load_weight_half(nc, words, plane, W2_words, W2_scales, source_half, half, g
                 )
 
 
+def load_weight_quarter(nc, words, plane, W2_words, W2_scales, group, source_half, half, side):
+    nc.sync.dma_start(
+        out=words[HALF * half : HALF * (half + 1), 2 * CH * side : 2 * CH * (side + 1)].bitcast(I32),
+        in_=W2_words[group, HALF * source_half : HALF * (source_half + 1), :].bitcast(I32),
+    )
+    for quad in range(2):
+        first = HALF * half + 32 * quad
+        row = 8 * source_half + 4 * quad
+        nc.sync.dma_start(
+            out=plane[first : first + 4, CH * side : CH * (side + 1)].bitcast(I32),
+            in_=W2_scales[group, row : row + 4, :].bitcast(I32),
+        )
+
+
 def transpose_row_pairs(nc, bank, row_pairs, identity):
     for t in range(TILES_PER_BANK):
         for u in range(2):
@@ -65,7 +79,9 @@ def tile_differentiablelogicmachine_pa_t_kernel(tc, x1, x2, W2_words, W2_scales,
     block_pairs += [(p, p) for p in range(BLOCKS)]
     count = len(block_pairs)
 
-    with tc.tile_pool(name="const", bufs=1) as const, tc.tile_pool(name="rows", bufs=count) as rows_pool, tc.tile_pool(
+    with tc.tile_pool(name="const", bufs=1) as const, tc.tile_pool(name="rows", bufs=count - BLOCKS) as rows_pool, tc.tile_pool(
+        name="square", bufs=BLOCKS
+    ) as square_pool, tc.tile_pool(
         name="quant", bufs=2
     ) as quant_pool, tc.tile_pool(name="result", bufs=4) as result_pool, tc.psum_pool(
         name="flip", bufs=4
@@ -74,10 +90,21 @@ def tile_differentiablelogicmachine_pa_t_kernel(tc, x1, x2, W2_words, W2_scales,
         x2_grouped = {}
         x2_codes = {}
         x2_plane = {}
+        x2_straight = {}
+        x2_straight_codes = {}
+        x2_straight_plane = {}
         results = {}
 
         def load_block_pair(n):
             p, q = block_pairs[n]
+            if p == q:
+                square = square_pool.tile([P, BLOCK + 1, CH], BF16)
+                nc.gpsimd.memset(square[:, BLOCK, :], 0.0)
+                nc.sync.dma_start(
+                    out=square[:, 0:BLOCK, :], in_=x2[:, BLOCK * p : BLOCK * (p + 1), BLOCK * p : BLOCK * (p + 1), :]
+                )
+                x2_rows[n] = square
+                return
             rows = rows_pool.tile([P, BLOCK, 2, CH], BF16)
             for d in range(BLOCK):
                 i0, j = BLOCK * p, BLOCK * q + d
@@ -88,6 +115,9 @@ def tile_differentiablelogicmachine_pa_t_kernel(tc, x1, x2, W2_words, W2_scales,
         def flip_block_pair(n):
             rows = x2_rows[n]
             grouped = quant_pool.tile([P, BLOCK, P, 4], BF16, align_bytes=64)
+            if block_pairs[n][0] == block_pairs[n][1]:
+                flip_square(n, rows, grouped)
+                return
             for d0 in range(0, BLOCK, TILES_PER_BANK):
                 bank = flip_pool.tile([P, TILES_PER_BANK, 2, P], F32, tag="bank")
                 transpose_row_pairs(
@@ -102,7 +132,33 @@ def tile_differentiablelogicmachine_pa_t_kernel(tc, x1, x2, W2_words, W2_scales,
                 )
             x2_grouped[n] = grouped
 
+        def flip_square(n, square, mirrored):
+            words = square[:].rearrange("c y k -> c (y k)").bitcast(F32)
+            straight = quant_pool.tile([P, BLOCK // 2, P, 4], BF16, align_bytes=64)
+            for e in range(BLOCK // 2):
+                bank = flip_pool.tile([P, TILES_PER_BANK, 2, P], F32, tag="bank")
+                transpose_row_pairs(
+                    nc, bank, [words[:, WORDS * (2 * e + t) : WORDS * (2 * e + t + 2)] for t in range(TILES_PER_BANK)], identity
+                )
+                nc.vector.tensor_copy(out=straight[:, e, :, :].bitcast(F32), in_=bank[:, 0, :, :].rearrange("n u c -> n c u"))
+                nc.scalar.copy(
+                    out=mirrored[:].bitcast(F32).rearrange("n d (b a) u -> n d b (a u)", a=BLOCK)[:, :, :, 4 * e : 4 * e + 4],
+                    in_=bank[:].rearrange("n t u (b x) -> n x b (t u)", x=BLOCK),
+                )
+            x2_grouped[n] = mirrored
+            x2_straight[n] = straight
+
         def quantise_block_pair(n):
+            if n in x2_straight:
+                straight_codes = quant_pool.tile([P, BLOCK // 2, P], U32, align_bytes=64)
+                straight_plane = quant_pool.tile([P, BLOCK // 2, P], U8, align_bytes=64)
+                nc.vector.quantize_mx(
+                    out=straight_codes[:].rearrange("n d c -> n (d c)").bitcast(FP8X4),
+                    scales=straight_plane[:].rearrange("n d c -> n (d c)"),
+                    in_=x2_straight[n][:].rearrange("n d c t -> n (d c t)"),
+                )
+                x2_straight_codes[n] = straight_codes
+                x2_straight_plane[n] = straight_plane
             grouped = x2_grouped[n]
             codes = quant_pool.tile([P, BLOCK, P], U32, align_bytes=64)
             plane = quant_pool.tile([P, BLOCK, P], U8, align_bytes=64)
@@ -123,6 +179,9 @@ def tile_differentiablelogicmachine_pa_t_kernel(tc, x1, x2, W2_words, W2_scales,
             if d0 == 0:
                 result = result_pool.tile([P, 2, BLOCK, CH], F32)
                 results[n] = result
+            if p == q:
+                multiply_square(n, d0)
+                return
             for d in range(d0, d0 + TILES_PER_STEP):
                 acc = acc_pool.tile([P, 2 * CH], F32, tag="acc")
                 for c0 in range(first * CH, 2 * CH, width):
@@ -148,6 +207,47 @@ def tile_differentiablelogicmachine_pa_t_kernel(tc, x1, x2, W2_words, W2_scales,
                     out=results[n][:, first:2, d, :],
                     in0=acc[:, first * CH : 2 * CH].rearrange("c (s o) -> c s o", o=CH),
                     in1=own[:, p, first * CH : 2 * CH].rearrange("c (s o) -> c s o", o=CH),
+                    op=ADD,
+                )
+
+        def multiply_square(n, d0):
+            p = block_pairs[n][0]
+            for e in range(d0 // 2, (d0 + TILES_PER_STEP) // 2):
+                acc = acc_pool.tile([P, 2 * CH], F32, tag="acc")
+                for c0 in range(0, 2 * CH, CH // 2):
+                    d = 2 * e + c0 // CH
+                    o0 = c0 % CH
+                    nc.tensor.matmul_mx(
+                        out=acc[:, c0 : c0 + CH // 2],
+                        lhsT=x2_straight_codes[n][:, e, :].bitcast(FP8X4),
+                        lhsT_scale=x2_straight_plane[n][:, e, :],
+                        rhs=w_straight[:, 2 * c0 : 2 * c0 + CH].bitcast(FP4X4),
+                        rhs_scale=s_straight[:, c0 : c0 + CH // 2],
+                        start=True,
+                        stop=False,
+                    )
+                    nc.tensor.matmul_mx(
+                        out=acc[:, c0 : c0 + CH // 2],
+                        lhsT=x2_codes[n][:, d, :].bitcast(FP8X4),
+                        lhsT_scale=x2_plane[n][:, d, :],
+                        rhs=w_mirrored[:, 2 * o0 : 2 * o0 + CH].bitcast(FP4X4),
+                        rhs_scale=s_mirrored[:, o0 : o0 + CH // 2],
+                        start=False,
+                        stop=False,
+                    )
+                    nc.tensor.matmul_mx(
+                        out=acc[:, c0 : c0 + CH // 2],
+                        lhsT=rep_codes[:, BLOCK * (p // 2) + d, :].bitcast(FP8X4),
+                        lhsT_scale=rep_plane[:, BLOCK * (p // 2) + d, :],
+                        rhs=w_x1[p % 2][:, 2 * (CH + o0) : 2 * (CH + o0) + CH].bitcast(FP4X4),
+                        rhs_scale=s_x1[p % 2][:, CH + o0 : CH + o0 + CH // 2],
+                        start=False,
+                        stop=True,
+                    )
+                nc.vector.tensor_tensor(
+                    out=results[n][:, 1, 2 * e : 2 * e + 2, :],
+                    in0=acc[:].rearrange("c (s o) -> c s o", o=CH),
+                    in1=own[:, p : p + 1, CH : 2 * CH].to_broadcast([P, 2, CH]),
                     op=ADD,
                 )
 
@@ -178,6 +278,12 @@ def tile_differentiablelogicmachine_pa_t_kernel(tc, x1, x2, W2_words, W2_scales,
             nc.vector.memset(w_x1[h][:].bitcast(I32), 0)
             nc.vector.memset(s_x1[h][:].bitcast(I32), 0)
         nc.vector.memset(s_x2[:].bitcast(I32), 0)
+        w_straight = const.tile([P, 4 * CH], U8, align_bytes=64)
+        s_straight = const.tile([P, 2 * CH], U8, align_bytes=64)
+        w_mirrored = const.tile([P, 2 * CH], U8, align_bytes=64)
+        s_mirrored = const.tile([P, CH], U8, align_bytes=64)
+        for zeroed in (w_straight, s_straight, w_mirrored, s_mirrored):
+            nc.vector.memset(zeroed[:].bitcast(I32), 0)
         b2_row = const.tile([P, CH], BF16)
         nc.vector.memset(b2_row[:], 0.0)
         ones = const.tile([P, P], BF16)
@@ -190,6 +296,9 @@ def tile_differentiablelogicmachine_pa_t_kernel(tc, x1, x2, W2_words, W2_scales,
         load_weight_half(nc, w_x2, s_x2, W2_words, W2_scales, 1, 1, (0, 1))
         for n in range(1, LOADS_AHEAD):
             load_block_pair(n)
+        load_weight_quarter(nc, w_straight, s_straight, W2_words, W2_scales, 0, 1, 0, 0)
+        load_weight_quarter(nc, w_straight, s_straight, W2_words, W2_scales, 0, 1, 1, 1)
+        load_weight_quarter(nc, w_mirrored, s_mirrored, W2_words, W2_scales, 1, 1, 0, 0)
 
         identity = const.tile([P, P], F32)
         make_identity(nc, identity[:])

@@ -258,7 +258,8 @@ def tile_differentiablelogicmachine_pa_t_kernel(tc, x1, x2, W2_words, W2_scales,
             d1 = d0 + TILES_PER_STEP
             done = results[n][:, first:2, d0:d1, :]
             nc.scalar.activation(out=done, in_=done, func=SIGMOID)
-            nc.gpsimd.dma_start(
+            large_queue = nc.gpsimd if q > p else nc.sync
+            large_queue.dma_start(
                 out=out[:, i0 : i0 + BLOCK, j0 + d0 : j0 + d1, :].rearrange("b a j o -> b a (j o)"),
                 in_=results[n][:, 1, d0:d1, :].rearrange("c j o -> c (j o)"),
             )

@@ -258,8 +258,7 @@ def tile_differentiablelogicmachine_pa_t_kernel(tc, x1, x2, W2_words, W2_scales,
             d1 = d0 + TILES_PER_STEP
             done = results[n][:, first:2, d0:d1, :]
             nc.scalar.activation(out=done, in_=done, func=SIGMOID)
-            large_queue = nc.gpsimd if q > p else nc.sync
-            large_queue.dma_start(
+            nc.sync.dma_start(
                 out=out[:, i0 : i0 + BLOCK, j0 + d0 : j0 + d1, :].rearrange("b a j o -> b a (j o)"),
                 in_=results[n][:, 1, d0:d1, :].rearrange("c j o -> c (j o)"),
             )

@@ -53,20 +53,6 @@ def load_weight_half(nc, words, plane, W2_words, W2_scales, source_half, half, g
                 )
 
 
-def load_weight_quarter(nc, words, plane, W2_words, W2_scales, group, source_half, half, side):
-    nc.sync.dma_start(
-        out=words[HALF * half : HALF * (half + 1), 2 * CH * side : 2 * CH * (side + 1)].bitcast(I32),
-        in_=W2_words[group, HALF * source_half : HALF * (source_half + 1), :].bitcast(I32),
-    )
-    for quad in range(2):
-        first = HALF * half + 32 * quad
-        row = 8 * source_half + 4 * quad
-        nc.sync.dma_start(
-            out=plane[first : first + 4, CH * side : CH * (side + 1)].bitcast(I32),
-            in_=W2_scales[group, row : row + 4, :].bitcast(I32),
-        )
-
-
 def transpose_row_pairs(nc, bank, row_pairs, identity):
     for t in range(TILES_PER_BANK):
         for u in range(2):
@@ -258,10 +244,16 @@ def tile_differentiablelogicmachine_pa_t_kernel(tc, x1, x2, W2_words, W2_scales,
             d1 = d0 + TILES_PER_STEP
             done = results[n][:, first:2, d0:d1, :]
             nc.scalar.activation(out=done, in_=done, func=SIGMOID)
-            nc.sync.dma_start(
-                out=out[:, i0 : i0 + BLOCK, j0 + d0 : j0 + d1, :].rearrange("b a j o -> b a (j o)"),
-                in_=results[n][:, 1, d0:d1, :].rearrange("c j o -> c (j o)"),
-            )
+            if n == count - 1:
+                nc.sync.dma_start(
+                    out=out[:, i0 : i0 + BLOCK, j0 + d0 : j0 + d1, :].rearrange("b a j o -> b a (j o)"),
+                    in_=results[n][:, 1, d0:d1, :].rearrange("c j o -> c (j o)"),
+                )
+            elif d1 == BLOCK:
+                nc.sync.dma_start(
+                    out=out[:, i0 : i0 + BLOCK, j0 : j0 + BLOCK, :].rearrange("b a j o -> b a (j o)"),
+                    in_=results[n][:, 1, :, :].rearrange("c j o -> c (j o)"),
+                )
             if q > p:
                 for d in range(d0, d1):
                     nc.sync.dma_start(out=out[:, j0 + d, i0 : i0 + BLOCK, :], in_=results[n][:, 0, d, :])
@@ -296,9 +288,12 @@ def tile_differentiablelogicmachine_pa_t_kernel(tc, x1, x2, W2_words, W2_scales,
         load_weight_half(nc, w_x2, s_x2, W2_words, W2_scales, 1, 1, (0, 1))
         for n in range(1, LOADS_AHEAD):
             load_block_pair(n)
-        load_weight_quarter(nc, w_straight, s_straight, W2_words, W2_scales, 0, 1, 0, 0)
-        load_weight_quarter(nc, w_straight, s_straight, W2_words, W2_scales, 0, 1, 1, 1)
-        load_weight_quarter(nc, w_mirrored, s_mirrored, W2_words, W2_scales, 1, 1, 0, 0)
+        upper, lower = slice(0, HALF), slice(HALF, P)
+        for target, source, width in ((w_straight, w_x2, 2 * CH), (s_straight, s_x2, CH)):
+            nc.gpsimd.tensor_copy(out=target[upper, 0:width].bitcast(I32), in_=source[upper, width : 2 * width].bitcast(I32))
+            nc.gpsimd.tensor_copy(out=target[lower, width : 2 * width].bitcast(I32), in_=source[lower, 0:width].bitcast(I32))
+        nc.gpsimd.tensor_copy(out=w_mirrored[upper, :].bitcast(I32), in_=w_x2[upper, 0 : 2 * CH].bitcast(I32))
+        nc.gpsimd.tensor_copy(out=s_mirrored[upper, :].bitcast(I32), in_=s_x2[upper, 0:CH].bitcast(I32))
 
         identity = const.tile([P, P], F32)
         make_identity(nc, identity[:])

@@ -92,10 +92,12 @@ def tile_differentiablelogicmachine_pa_t_kernel(tc, x1, x2, W2_words, W2_scales,
                 x2_rows[n] = square
                 return
             rows = rows_pool.tile([P, BLOCK, 2, CH], BF16)
-            for d in range(BLOCK):
-                i0, j = BLOCK * p, BLOCK * q + d
-                nc.sync.dma_start(out=rows[:, d, 0, :], in_=x2[:, i0 : i0 + BLOCK, j, :])
-                nc.sync.dma_start(out=rows[:, d, 1, :], in_=x2[:, j, i0 : i0 + BLOCK, :])
+            places = rows[:].rearrange("c d h k -> c (d h) k")
+            i0, j0 = BLOCK * p, BLOCK * q
+            for d in range(0, BLOCK, 2):
+                nc.sync.dma_start(out=places[:, 2 * d, :], in_=x2[:, j0 + d, i0 : i0 + BLOCK, :])
+                nc.sync.dma_start(out=places[:, 2 * d + 1 : 2 * d + 3, :], in_=x2[:, i0 : i0 + BLOCK, j0 + d : j0 + d + 2, :])
+                nc.sync.dma_start(out=places[:, 2 * d + 3, :], in_=x2[:, j0 + d + 1, i0 : i0 + BLOCK, :])
             x2_rows[n] = rows
 
         def flip_block_pair(n):
@@ -175,8 +177,8 @@ def tile_differentiablelogicmachine_pa_t_kernel(tc, x1, x2, W2_words, W2_scales,
                         out=acc[:, c0 : c0 + width],
                         lhsT=x2_codes[n][:, d, :].bitcast(FP8X4),
                         lhsT_scale=x2_plane[n][:, d, :],
-                        rhs=w_x2[:, 2 * c0 : 2 * (c0 + width)].bitcast(FP4X4),
-                        rhs_scale=s_x2[:, c0 : c0 + width],
+                        rhs=w_x2_by_order[d % 2][:, 2 * c0 : 2 * (c0 + width)].bitcast(FP4X4),
+                        rhs_scale=s_x2_by_order[d % 2][:, c0 : c0 + width],
                         start=True,
                         stop=False,
                     )
@@ -258,6 +260,9 @@ def tile_differentiablelogicmachine_pa_t_kernel(tc, x1, x2, W2_words, W2_scales,
                 for d in range(d0, d1):
                     nc.sync.dma_start(out=out[:, j0 + d, i0 : i0 + BLOCK, :], in_=results[n][:, 0, d, :])
 
+        identity = const.tile([P, P], F32)
+        make_identity(nc, identity[:])
+
         x1_rows = const.tile([P, BLOCKS, CH], BF16)
         for p in range(BLOCKS):
             nc.sync.dma_start(out=x1_rows[:, p, :], in_=x1[:, BLOCK * p : BLOCK * (p + 1), :])
@@ -288,6 +293,13 @@ def tile_differentiablelogicmachine_pa_t_kernel(tc, x1, x2, W2_words, W2_scales,
         load_weight_half(nc, w_x2, s_x2, W2_words, W2_scales, 1, 1, (0, 1))
         for n in range(1, LOADS_AHEAD):
             load_block_pair(n)
+        w_x2_swapped = const.tile([P, 4 * CH], U8, align_bytes=64)
+        s_x2_swapped = const.tile([P, 2 * CH], U8, align_bytes=64)
+        for target, source, width in ((w_x2_swapped, w_x2, 2 * CH), (s_x2_swapped, s_x2, CH)):
+            nc.gpsimd.tensor_copy(out=target[:, 0:width].bitcast(I32), in_=source[:, width : 2 * width].bitcast(I32))
+            nc.gpsimd.tensor_copy(out=target[:, width : 2 * width].bitcast(I32), in_=source[:, 0:width].bitcast(I32))
+        w_x2_by_order = (w_x2_swapped, w_x2)
+        s_x2_by_order = (s_x2_swapped, s_x2)
         upper, lower = slice(0, HALF), slice(HALF, P)
         for target, source, width in ((w_straight, w_x2, 2 * CH), (s_straight, s_x2, CH)):
             nc.gpsimd.tensor_copy(out=target[upper, 0:width].bitcast(I32), in_=source[upper, width : 2 * width].bitcast(I32))
@@ -295,8 +307,6 @@ def tile_differentiablelogicmachine_pa_t_kernel(tc, x1, x2, W2_words, W2_scales,
         nc.gpsimd.tensor_copy(out=w_mirrored[upper, :].bitcast(I32), in_=w_x2[upper, 0 : 2 * CH].bitcast(I32))
         nc.gpsimd.tensor_copy(out=s_mirrored[upper, :].bitcast(I32), in_=s_x2[upper, 0:CH].bitcast(I32))
 
-        identity = const.tile([P, P], F32)
-        make_identity(nc, identity[:])
         warm = const.tile([P, 1], F32)
         nc.vector.memset(warm[:], 0.0)
         nc.scalar.activation(out=warm[:], in_=warm[:], func=SIGMOID)

@@ -246,16 +246,10 @@ def tile_differentiablelogicmachine_pa_t_kernel(tc, x1, x2, W2_words, W2_scales,
             d1 = d0 + TILES_PER_STEP
             done = results[n][:, first:2, d0:d1, :]
             nc.scalar.activation(out=done, in_=done, func=SIGMOID)
-            if n == count - 1:
-                nc.sync.dma_start(
-                    out=out[:, i0 : i0 + BLOCK, j0 + d0 : j0 + d1, :].rearrange("b a j o -> b a (j o)"),
-                    in_=results[n][:, 1, d0:d1, :].rearrange("c j o -> c (j o)"),
-                )
-            elif d1 == BLOCK:
-                nc.sync.dma_start(
-                    out=out[:, i0 : i0 + BLOCK, j0 : j0 + BLOCK, :].rearrange("b a j o -> b a (j o)"),
-                    in_=results[n][:, 1, :, :].rearrange("c j o -> c (j o)"),
-                )
+            nc.sync.dma_start(
+                out=out[:, i0 : i0 + BLOCK, j0 + d0 : j0 + d1, :].rearrange("b a j o -> b a (j o)"),
+                in_=results[n][:, 1, d0:d1, :].rearrange("c j o -> c (j o)"),
+            )
             if q > p:
                 for d in range(d0, d1):
                     nc.sync.dma_start(out=out[:, j0 + d, i0 : i0 + BLOCK, :], in_=results[n][:, 0, d, :])

@@ -76,19 +76,17 @@ def tile_differentiablelogicmachine_pa_t_kernel(tc, x1, x2, W2_words, W2_scales,
         x2_grouped = {}
         x2_codes = {}
         x2_plane = {}
-        x2_straight = {}
-        x2_straight_codes = {}
-        x2_straight_plane = {}
         results = {}
 
         def load_block_pair(n):
             p, q = block_pairs[n]
             if p == q:
                 square = square_pool.tile([P, BLOCK + 1, CH], BF16)
-                nc.gpsimd.memset(square[:, BLOCK, :], 0.0)
                 nc.sync.dma_start(
-                    out=square[:, 0:BLOCK, :], in_=x2[:, BLOCK * p : BLOCK * (p + 1), BLOCK * p : BLOCK * (p + 1), :]
+                    out=square[:, 1 : BLOCK + 1, :],
+                    in_=x2[:, BLOCK * p : BLOCK * (p + 1), BLOCK * p : BLOCK * (p + 1), :],
                 )
+                nc.gpsimd.tensor_copy(out=square[:, 0, :], in_=square[:, BLOCK, :])
                 x2_rows[n] = square
                 return
             rows = rows_pool.tile([P, BLOCK, 2, CH], BF16)
@@ -120,33 +118,29 @@ def tile_differentiablelogicmachine_pa_t_kernel(tc, x1, x2, W2_words, W2_scales,
                 )
             x2_grouped[n] = grouped
 
-        def flip_square(n, square, mirrored):
+        def flip_square(n, square, grouped):
             words = square[:].rearrange("c y k -> c (y k)").bitcast(F32)
-            straight = quant_pool.tile([P, BLOCK // 2, P, 4], BF16, align_bytes=64)
+            upper, lower = slice(0, HALF), slice(HALF, P)
+            by_tile = grouped[:].bitcast(F32)
             for e in range(BLOCK // 2):
                 bank = flip_pool.tile([P, TILES_PER_BANK, 2, P], F32, tag="bank")
                 transpose_row_pairs(
                     nc, bank, [words[:, WORDS * (2 * e + t) : WORDS * (2 * e + t + 2)] for t in range(TILES_PER_BANK)], identity
                 )
-                nc.vector.tensor_copy(out=straight[:, e, :, :].bitcast(F32), in_=bank[:, 0, :, :].rearrange("n u c -> n c u"))
-                nc.scalar.copy(
-                    out=mirrored[:].bitcast(F32).rearrange("n d (b a) u -> n d b (a u)", a=BLOCK)[:, :, :, 4 * e : 4 * e + 4],
-                    in_=bank[:].rearrange("n t u (b x) -> n x b (t u)", x=BLOCK),
+                copy = nc.scalar.copy if e % 2 == 0 else nc.vector.tensor_copy
+                as_it_is = bank[upper].rearrange("n t u c -> n t c u")
+                if e == 0:
+                    copy(out=by_tile[upper, BLOCK - 1, :, :], in_=as_it_is[:, 0, :, :])
+                    copy(out=by_tile[upper, 0, :, :], in_=as_it_is[:, 1, :, :])
+                else:
+                    copy(out=by_tile[upper, 2 * e - 1 : 2 * e + 1, :, :], in_=as_it_is)
+                copy(
+                    out=by_tile[lower].rearrange("n d (b a) u -> n d b (a u)", a=BLOCK)[:, :, :, 4 * e : 4 * e + 4],
+                    in_=bank[lower].rearrange("n t u (b x) -> n x b (t u)", x=BLOCK),
                 )
-            x2_grouped[n] = mirrored
-            x2_straight[n] = straight
+            x2_grouped[n] = grouped
 
         def quantise_block_pair(n):
-            if n in x2_straight:
-                straight_codes = quant_pool.tile([P, BLOCK // 2, P], U32, align_bytes=64)
-                straight_plane = quant_pool.tile([P, BLOCK // 2, P], U8, align_bytes=64)
-                nc.vector.quantize_mx(
-                    out=straight_codes[:].rearrange("n d c -> n (d c)").bitcast(FP8X4),
-                    scales=straight_plane[:].rearrange("n d c -> n (d c)"),
-                    in_=x2_straight[n][:].rearrange("n d c t -> n (d c t)"),
-                )
-                x2_straight_codes[n] = straight_codes
-                x2_straight_plane[n] = straight_plane
             grouped = x2_grouped[n]
             codes = quant_pool.tile([P, BLOCK, P], U32, align_bytes=64)
             plane = quant_pool.tile([P, BLOCK, P], U8, align_bytes=64)
@@ -162,8 +156,6 @@ def tile_differentiablelogicmachine_pa_t_kernel(tc, x1, x2, W2_words, W2_scales,
 
         def multiply_step(n, d0):
             p, q = block_pairs[n]
-            first = 0 if q > p else 1
-            width = 2 * CH if q > p else CH // 2
             if d0 == 0:
                 result = result_pool.tile([P, 2, BLOCK, CH], F32)
                 results[n] = result
@@ -172,29 +164,28 @@ def tile_differentiablelogicmachine_pa_t_kernel(tc, x1, x2, W2_words, W2_scales,
                 return
             for d in range(d0, d0 + TILES_PER_STEP):
                 acc = acc_pool.tile([P, 2 * CH], F32, tag="acc")
-                for c0 in range(first * CH, 2 * CH, width):
-                    nc.tensor.matmul_mx(
-                        out=acc[:, c0 : c0 + width],
-                        lhsT=x2_codes[n][:, d, :].bitcast(FP8X4),
-                        lhsT_scale=x2_plane[n][:, d, :],
-                        rhs=w_x2_by_order[d % 2][:, 2 * c0 : 2 * (c0 + width)].bitcast(FP4X4),
-                        rhs_scale=s_x2_by_order[d % 2][:, c0 : c0 + width],
-                        start=True,
-                        stop=False,
-                    )
-                    nc.tensor.matmul_mx(
-                        out=acc[:, c0 : c0 + width],
-                        lhsT=rep_codes[:, BLOCK * (q // 2) + d, :].bitcast(FP8X4),
-                        lhsT_scale=rep_plane[:, BLOCK * (q // 2) + d, :],
-                        rhs=w_x1[q % 2][:, 2 * c0 : 2 * (c0 + width)].bitcast(FP4X4),
-                        rhs_scale=s_x1[q % 2][:, c0 : c0 + width],
-                        start=False,
-                        stop=True,
-                    )
+                nc.tensor.matmul_mx(
+                    out=acc[:],
+                    lhsT=x2_codes[n][:, d, :].bitcast(FP8X4),
+                    lhsT_scale=x2_plane[n][:, d, :],
+                    rhs=w_x2_by_order[d % 2][:].bitcast(FP4X4),
+                    rhs_scale=s_x2_by_order[d % 2][:],
+                    start=True,
+                    stop=False,
+                )
+                nc.tensor.matmul_mx(
+                    out=acc[:],
+                    lhsT=rep_codes[:, BLOCK * (q // 2) + d, :].bitcast(FP8X4),
+                    lhsT_scale=rep_plane[:, BLOCK * (q // 2) + d, :],
+                    rhs=w_x1[q % 2][:].bitcast(FP4X4),
+                    rhs_scale=s_x1[q % 2][:],
+                    start=False,
+                    stop=True,
+                )
                 nc.vector.tensor_tensor(
-                    out=results[n][:, first:2, d, :],
-                    in0=acc[:, first * CH : 2 * CH].rearrange("c (s o) -> c s o", o=CH),
-                    in1=own[:, p, first * CH : 2 * CH].rearrange("c (s o) -> c s o", o=CH),
+                    out=results[n][:, :, d, :],
+                    in0=acc[:].rearrange("c (s o) -> c s o", o=CH),
+                    in1=own[:, p, :].rearrange("c (s o) -> c s o", o=CH),
                     op=ADD,
                 )
 
@@ -204,31 +195,24 @@ def tile_differentiablelogicmachine_pa_t_kernel(tc, x1, x2, W2_words, W2_scales,
                 acc = acc_pool.tile([P, 2 * CH], F32, tag="acc")
                 for c0 in range(0, 2 * CH, CH // 2):
                     d = 2 * e + c0 // CH
-                    o0 = c0 % CH
-                    nc.tensor.matmul_mx(
-                        out=acc[:, c0 : c0 + CH // 2],
-                        lhsT=x2_straight_codes[n][:, e, :].bitcast(FP8X4),
-                        lhsT_scale=x2_straight_plane[n][:, e, :],
-                        rhs=w_straight[:, 2 * c0 : 2 * c0 + CH].bitcast(FP4X4),
-                        rhs_scale=s_straight[:, c0 : c0 + CH // 2],
-                        start=True,
-                        stop=False,
-                    )
+                    o0 = CH + c0 % CH
+                    cols = slice(o0, o0 + CH // 2)
+                    words = slice(2 * o0, 2 * o0 + CH)
                     nc.tensor.matmul_mx(
                         out=acc[:, c0 : c0 + CH // 2],
                         lhsT=x2_codes[n][:, d, :].bitcast(FP8X4),
                         lhsT_scale=x2_plane[n][:, d, :],
-                        rhs=w_mirrored[:, 2 * o0 : 2 * o0 + CH].bitcast(FP4X4),
-                        rhs_scale=s_mirrored[:, o0 : o0 + CH // 2],
-                        start=False,
+                        rhs=w_x2[:, words].bitcast(FP4X4),
+                        rhs_scale=s_x2[:, cols],
+                        start=True,
                         stop=False,
                     )
                     nc.tensor.matmul_mx(
                         out=acc[:, c0 : c0 + CH // 2],
                         lhsT=rep_codes[:, BLOCK * (p // 2) + d, :].bitcast(FP8X4),
                         lhsT_scale=rep_plane[:, BLOCK * (p // 2) + d, :],
-                        rhs=w_x1[p % 2][:, 2 * (CH + o0) : 2 * (CH + o0) + CH].bitcast(FP4X4),
-                        rhs_scale=s_x1[p % 2][:, CH + o0 : CH + o0 + CH // 2],
+                        rhs=w_x1[p % 2][:, words].bitcast(FP4X4),
+                        rhs_scale=s_x1[p % 2][:, cols],
                         start=False,
                         stop=True,
                     )
@@ -269,12 +253,6 @@ def tile_differentiablelogicmachine_pa_t_kernel(tc, x1, x2, W2_words, W2_scales,
             nc.vector.memset(w_x1[h][:].bitcast(I32), 0)
             nc.vector.memset(s_x1[h][:].bitcast(I32), 0)
         nc.vector.memset(s_x2[:].bitcast(I32), 0)
-        w_straight = const.tile([P, 4 * CH], U8, align_bytes=64)
-        s_straight = const.tile([P, 2 * CH], U8, align_bytes=64)
-        w_mirrored = const.tile([P, 2 * CH], U8, align_bytes=64)
-        s_mirrored = const.tile([P, CH], U8, align_bytes=64)
-        for zeroed in (w_straight, s_straight, w_mirrored, s_mirrored):
-            nc.vector.memset(zeroed[:].bitcast(I32), 0)
         b2_row = const.tile([P, CH], BF16)
         nc.vector.memset(b2_row[:], 0.0)
         ones = const.tile([P, P], BF16)
@@ -294,13 +272,6 @@ def tile_differentiablelogicmachine_pa_t_kernel(tc, x1, x2, W2_words, W2_scales,
             nc.gpsimd.tensor_copy(out=target[:, width : 2 * width].bitcast(I32), in_=source[:, 0:width].bitcast(I32))
         w_x2_by_order = (w_x2_swapped, w_x2)
         s_x2_by_order = (s_x2_swapped, s_x2)
-        upper, lower = slice(0, HALF), slice(HALF, P)
-        for target, source, width in ((w_straight, w_x2, 2 * CH), (s_straight, s_x2, CH)):
-            nc.gpsimd.tensor_copy(out=target[upper, 0:width].bitcast(I32), in_=source[upper, width : 2 * width].bitcast(I32))
-            nc.gpsimd.tensor_copy(out=target[lower, width : 2 * width].bitcast(I32), in_=source[lower, 0:width].bitcast(I32))
-        nc.gpsimd.tensor_copy(out=w_mirrored[upper, :].bitcast(I32), in_=w_x2[upper, 0 : 2 * CH].bitcast(I32))
-        nc.gpsimd.tensor_copy(out=s_mirrored[upper, :].bitcast(I32), in_=s_x2[upper, 0:CH].bitcast(I32))
-
         warm = const.tile([P, 1], F32)
         nc.vector.memset(warm[:], 0.0)
         nc.scalar.activation(out=warm[:], in_=warm[:], func=SIGMOID)

@@ -86,7 +86,7 @@ def tile_differentiablelogicmachine_pa_t_kernel(tc, x1, x2, W2_words, W2_scales,
                     out=square[:, 1 : BLOCK + 1, :],
                     in_=x2[:, BLOCK * p : BLOCK * (p + 1), BLOCK * p : BLOCK * (p + 1), :],
                 )
-                nc.gpsimd.tensor_copy(out=square[:, 0, :], in_=square[:, BLOCK, :])
+                nc.sync.dma_start(out=square[:, 0, :], in_=x2[:, BLOCK * p : BLOCK * (p + 1), BLOCK * (p + 1) - 1, :])
                 x2_rows[n] = square
                 return
             rows = rows_pool.tile([P, BLOCK, 2, CH], BF16)
@@ -135,8 +135,8 @@ def tile_differentiablelogicmachine_pa_t_kernel(tc, x1, x2, W2_words, W2_scales,
                 else:
                     copy(out=by_tile[upper, 2 * e - 1 : 2 * e + 1, :, :], in_=as_it_is)
                 copy(
-                    out=by_tile[lower].rearrange("n d (b a) u -> n d b (a u)", a=BLOCK)[:, :, :, 4 * e : 4 * e + 4],
-                    in_=bank[lower].rearrange("n t u (b x) -> n x b (t u)", x=BLOCK),
+                    out=by_tile[lower].rearrange("n d (b a) u -> n b d (a u)", a=BLOCK)[:, :, :, 4 * e : 4 * e + 4],
+                    in_=bank[lower].rearrange("n t u (b x) -> n b x (t u)", x=BLOCK),
                 )
             x2_grouped[n] = grouped
 

@@ -20,36 +20,39 @@ BLOCK = 8
 BLOCKS = OBJECTS // BLOCK
 WORDS = CH // 2
 TILES_PER_BANK = 2
+FLIP_AHEAD = 3
+QUANTISE_AHEAD = 1
+END_TILES = 2
 TILES_PER_STEP = 4
 LOADS_AHEAD = 5
 
 FLOPS = 2 * SCENES * OBJECTS * OBJECTS * 4 * CH * CH
 
 
-def load_weight_half(nc, words, plane, W2_words, W2_scales, source_half, half, groups):
+def load_weight_half(nc, words, plane, W2_words, W2_scales, source_half, half, groups, todo):
     rows = slice(HALF * source_half, HALF * (source_half + 1))
     to = slice(HALF * half, HALF * (half + 1))
     if groups == (0, 1):
-        nc.sync.dma_start(out=words[to, :].bitcast(I32), in_=W2_words[:, rows, :].bitcast(I32).rearrange("g p n -> p g n"))
+        todo.append((words[to, :].bitcast(I32), W2_words[:, rows, :].bitcast(I32).rearrange("g p n -> p g n")))
     else:
         for side in range(2):
-            nc.sync.dma_start(
-                out=words[to, 2 * CH * side : 2 * CH * (side + 1)].bitcast(I32),
-                in_=W2_words[groups[side], rows, :].bitcast(I32),
+            todo.append(
+                (words[to, 2 * CH * side : 2 * CH * (side + 1)].bitcast(I32), W2_words[groups[side], rows, :].bitcast(I32))
             )
     for quad in range(2):
         first = HALF * half + 32 * quad
         row = 8 * source_half + 4 * quad
         if groups == (0, 1):
-            nc.sync.dma_start(
-                out=plane[first : first + 4, :].bitcast(I32),
-                in_=W2_scales[:, row : row + 4, :].bitcast(I32).rearrange("g r n -> r g n"),
+            todo.append(
+                (plane[first : first + 4, :].bitcast(I32), W2_scales[:, row : row + 4, :].bitcast(I32).rearrange("g r n -> r g n"))
             )
         else:
             for side in range(2):
-                nc.sync.dma_start(
-                    out=plane[first : first + 4, CH * side : CH * (side + 1)].bitcast(I32),
-                    in_=W2_scales[groups[side], row : row + 4, :].bitcast(I32),
+                todo.append(
+                    (
+                        plane[first : first + 4, CH * side : CH * (side + 1)].bitcast(I32),
+                        W2_scales[groups[side], row : row + 4, :].bitcast(I32),
+                    )
                 )
 
 
@@ -61,8 +64,7 @@ def transpose_row_pairs(nc, bank, row_pairs, identity):
 
 def tile_differentiablelogicmachine_pa_t_kernel(tc, x1, x2, W2_words, W2_scales, b2, out):
     nc = tc.nc
-    block_pairs = [(p, q) for p in range(BLOCKS) for q in range(p + 1, BLOCKS)]
-    block_pairs += [(p, p) for p in range(BLOCKS)]
+    block_pairs = [(0, 0)] + [(p, q) for p in range(BLOCKS) for q in range(p + 1, BLOCKS)] + [(p, p) for p in range(1, BLOCKS)]
     count = len(block_pairs)
 
     with tc.tile_pool(name="const", bufs=1) as const, tc.tile_pool(name="rows", bufs=count - BLOCKS) as rows_pool, tc.tile_pool(
@@ -78,33 +80,40 @@ def tile_differentiablelogicmachine_pa_t_kernel(tc, x1, x2, W2_words, W2_scales,
         x2_plane = {}
         results = {}
 
-        def load_block_pair(n):
+        def block_pair_loads(n):
             p, q = block_pairs[n]
             if p == q:
                 square = square_pool.tile([P, BLOCK + 1, CH], BF16)
-                nc.sync.dma_start(
-                    out=square[:, 1 : BLOCK + 1, :],
-                    in_=x2[:, BLOCK * p : BLOCK * (p + 1), BLOCK * p : BLOCK * (p + 1), :],
-                )
-                nc.sync.dma_start(out=square[:, 0, :], in_=x2[:, BLOCK * p : BLOCK * (p + 1), BLOCK * (p + 1) - 1, :])
+                own_rows = slice(BLOCK * p, BLOCK * (p + 1))
                 x2_rows[n] = square
-                return
+                return [
+                    (square[:, 1 : BLOCK + 1, :], x2[:, own_rows, own_rows, :]),
+                    (square[:, 0, :], x2[:, own_rows, BLOCK * (p + 1) - 1, :]),
+                ]
             rows = rows_pool.tile([P, BLOCK, 2, CH], BF16)
             places = rows[:].rearrange("c d h k -> c (d h) k")
             i0, j0 = BLOCK * p, BLOCK * q
+            todo = []
             for d in range(0, BLOCK, 2):
-                nc.sync.dma_start(out=places[:, 2 * d, :], in_=x2[:, j0 + d, i0 : i0 + BLOCK, :])
-                nc.sync.dma_start(out=places[:, 2 * d + 1 : 2 * d + 3, :], in_=x2[:, i0 : i0 + BLOCK, j0 + d : j0 + d + 2, :])
-                nc.sync.dma_start(out=places[:, 2 * d + 3, :], in_=x2[:, j0 + d + 1, i0 : i0 + BLOCK, :])
+                todo.append((places[:, 2 * d, :], x2[:, j0 + d, i0 : i0 + BLOCK, :]))
+                todo.append((places[:, 2 * d + 1 : 2 * d + 3, :], x2[:, i0 : i0 + BLOCK, j0 + d : j0 + d + 2, :]))
+                todo.append((places[:, 2 * d + 3, :], x2[:, j0 + d + 1, i0 : i0 + BLOCK, :]))
             x2_rows[n] = rows
+            return todo
 
-        def flip_block_pair(n):
-            rows = x2_rows[n]
-            grouped = quant_pool.tile([P, BLOCK, P, 4], BF16, align_bytes=64)
+        def load_block_pair(n):
+            for target, source in block_pair_loads(n):
+                nc.sync.dma_start(out=target, in_=source)
+
+        def flip_half(n, h):
+            if h == 0:
+                x2_grouped[n] = quant_pool.tile([P, BLOCK, P, 4], BF16, name="grouped", align_bytes=64)
+            grouped = x2_grouped[n]
             if block_pairs[n][0] == block_pairs[n][1]:
-                flip_square(n, rows, grouped)
+                flip_square_half(n, h)
                 return
-            for d0 in range(0, BLOCK, TILES_PER_BANK):
+            rows = x2_rows[n]
+            for d0 in range(TILES_PER_STEP * h, TILES_PER_STEP * (h + 1), TILES_PER_BANK):
                 bank = flip_pool.tile([P, TILES_PER_BANK, 2, P], F32, tag="bank")
                 transpose_row_pairs(
                     nc,
@@ -116,43 +125,41 @@ def tile_differentiablelogicmachine_pa_t_kernel(tc, x1, x2, W2_words, W2_scales,
                     out=grouped[:, d0 : d0 + TILES_PER_BANK, :, :].bitcast(F32),
                     in_=bank[:].rearrange("n t u c -> n t c u"),
                 )
-            x2_grouped[n] = grouped
 
-        def flip_square(n, square, grouped):
-            words = square[:].rearrange("c y k -> c (y k)").bitcast(F32)
+        def flip_square_half(n, h):
+            grouped = x2_grouped[n]
+            words = x2_rows[n][:].rearrange("c y k -> c (y k)").bitcast(F32)
             upper, lower = slice(0, HALF), slice(HALF, P)
             by_tile = grouped[:].bitcast(F32)
-            for e in range(BLOCK // 2):
+            for e in range(2 * h, 2 * h + 2):
                 bank = flip_pool.tile([P, TILES_PER_BANK, 2, P], F32, tag="bank")
                 transpose_row_pairs(
                     nc, bank, [words[:, WORDS * (2 * e + t) : WORDS * (2 * e + t + 2)] for t in range(TILES_PER_BANK)], identity
                 )
-                copy = nc.scalar.copy if e % 2 == 0 else nc.vector.tensor_copy
+                copy = nc.vector.tensor_copy if e % 2 else nc.scalar.copy
+                copy_mirrored = nc.vector.tensor_copy if e == 3 else nc.scalar.copy
                 as_it_is = bank[upper].rearrange("n t u c -> n t c u")
                 if e == 0:
                     copy(out=by_tile[upper, BLOCK - 1, :, :], in_=as_it_is[:, 0, :, :])
                     copy(out=by_tile[upper, 0, :, :], in_=as_it_is[:, 1, :, :])
                 else:
                     copy(out=by_tile[upper, 2 * e - 1 : 2 * e + 1, :, :], in_=as_it_is)
-                copy(
+                copy_mirrored(
                     out=by_tile[lower].rearrange("n d (b a) u -> n b d (a u)", a=BLOCK)[:, :, :, 4 * e : 4 * e + 4],
                     in_=bank[lower].rearrange("n t u (b x) -> n b x (t u)", x=BLOCK),
                 )
-            x2_grouped[n] = grouped
 
-        def quantise_block_pair(n):
+        def quantise_half(n, h):
             grouped = x2_grouped[n]
-            codes = quant_pool.tile([P, BLOCK, P], U32, align_bytes=64)
-            plane = quant_pool.tile([P, BLOCK, P], U8, align_bytes=64)
-            for d0 in range(0, BLOCK, TILES_PER_STEP):
-                tiles = slice(d0, d0 + TILES_PER_STEP)
-                nc.vector.quantize_mx(
-                    out=codes[:, tiles, :].rearrange("n d c -> n (d c)").bitcast(FP8X4),
-                    scales=plane[:, tiles, :].rearrange("n d c -> n (d c)"),
-                    in_=grouped[:, tiles, :, :].rearrange("n d c t -> n (d c t)"),
-                )
-            x2_codes[n] = codes
-            x2_plane[n] = plane
+            if h == 0:
+                x2_codes[n] = quant_pool.tile([P, BLOCK, P], U32, name="codes", align_bytes=64)
+                x2_plane[n] = quant_pool.tile([P, BLOCK, P], U8, name="plane", align_bytes=64)
+            tiles = slice(TILES_PER_STEP * h, TILES_PER_STEP * (h + 1))
+            nc.vector.quantize_mx(
+                out=x2_codes[n][:, tiles, :].rearrange("n d c -> n (d c)").bitcast(FP8X4),
+                scales=x2_plane[n][:, tiles, :].rearrange("n d c -> n (d c)"),
+                in_=grouped[:, tiles, :, :].rearrange("n d c t -> n (d c t)"),
+            )
 
         def multiply_step(n, d0):
             p, q = block_pairs[n]
@@ -195,15 +202,17 @@ def tile_differentiablelogicmachine_pa_t_kernel(tc, x1, x2, W2_words, W2_scales,
                 acc = acc_pool.tile([P, 2 * CH], F32, tag="acc")
                 for c0 in range(0, 2 * CH, CH // 2):
                     d = 2 * e + c0 // CH
-                    o0 = CH + c0 % CH
+                    o0 = c0 % CH
                     cols = slice(o0, o0 + CH // 2)
                     words = slice(2 * o0, 2 * o0 + CH)
+                    x1_cols = slice(CH + o0, CH + o0 + CH // 2)
+                    x1_words = slice(2 * (CH + o0), 2 * (CH + o0) + CH)
                     nc.tensor.matmul_mx(
                         out=acc[:, c0 : c0 + CH // 2],
                         lhsT=x2_codes[n][:, d, :].bitcast(FP8X4),
                         lhsT_scale=x2_plane[n][:, d, :],
-                        rhs=w_x2[:, words].bitcast(FP4X4),
-                        rhs_scale=s_x2[:, cols],
+                        rhs=w_even[:, words].bitcast(FP4X4),
+                        rhs_scale=s_even[:, cols],
                         start=True,
                         stop=False,
                     )
@@ -211,8 +220,8 @@ def tile_differentiablelogicmachine_pa_t_kernel(tc, x1, x2, W2_words, W2_scales,
                         out=acc[:, c0 : c0 + CH // 2],
                         lhsT=rep_codes[:, BLOCK * (p // 2) + d, :].bitcast(FP8X4),
                         lhsT_scale=rep_plane[:, BLOCK * (p // 2) + d, :],
-                        rhs=w_x1[p % 2][:, words].bitcast(FP4X4),
-                        rhs_scale=s_x1[p % 2][:, cols],
+                        rhs=w_x1[p % 2][:, x1_words].bitcast(FP4X4),
+                        rhs_scale=s_x1[p % 2][:, x1_cols],
                         start=False,
                         stop=True,
                     )
@@ -223,11 +232,11 @@ def tile_differentiablelogicmachine_pa_t_kernel(tc, x1, x2, W2_words, W2_scales,
                     op=ADD,
                 )
 
-        def finish_step(n, d0):
+        def finish_step(n, d0, tiles=TILES_PER_STEP):
             p, q = block_pairs[n]
             first = 0 if q > p else 1
             i0, j0 = BLOCK * p, BLOCK * q
-            d1 = d0 + TILES_PER_STEP
+            d1 = d0 + tiles
             done = results[n][:, first:2, d0:d1, :]
             nc.scalar.activation(out=done, in_=done, func=SIGMOID)
             nc.sync.dma_start(
@@ -242,51 +251,46 @@ def tile_differentiablelogicmachine_pa_t_kernel(tc, x1, x2, W2_words, W2_scales,
         make_identity(nc, identity[:])
 
         x1_rows = const.tile([P, BLOCKS, CH], BF16)
-        for p in range(BLOCKS):
-            nc.sync.dma_start(out=x1_rows[:, p, :], in_=x1[:, BLOCK * p : BLOCK * (p + 1), :])
 
-        w_x2 = const.tile([P, 4 * CH], U8, align_bytes=64)
-        s_x2 = const.tile([P, 2 * CH], U8, align_bytes=64)
+        w_even = const.tile([P, 4 * CH], U8, align_bytes=64)
+        s_even = const.tile([P, 2 * CH], U8, align_bytes=64)
+        w_odd = const.tile([P, 4 * CH], U8, align_bytes=64)
+        s_odd = const.tile([P, 2 * CH], U8, align_bytes=64)
         w_x1 = [const.tile([P, 4 * CH], U8, name="w_x1_%d" % h, align_bytes=64) for h in range(2)]
         s_x1 = [const.tile([P, 2 * CH], U8, name="s_x1_%d" % h, align_bytes=64) for h in range(2)]
         for h in range(2):
             nc.vector.memset(w_x1[h][:].bitcast(I32), 0)
             nc.vector.memset(s_x1[h][:].bitcast(I32), 0)
-        nc.vector.memset(s_x2[:].bitcast(I32), 0)
+        nc.vector.memset(s_even[:].bitcast(I32), 0)
         b2_row = const.tile([P, CH], BF16)
         nc.vector.memset(b2_row[:], 0.0)
         ones = const.tile([P, P], BF16)
         nc.vector.memset(ones[:], 1.0)
+        def go(*todo):
+            for target, source in todo:
+                nc.sync.dma_start(out=target, in_=source)
+        small = [[], []]
         for h in range(2):
-            load_weight_half(nc, w_x1[h], s_x1[h], W2_words, W2_scales, 0, h, (0, 1))
-        nc.sync.dma_start(out=b2_row[0:1, :], in_=b2.rearrange("(x o) -> x o", x=1))
-        load_block_pair(0)
-        load_weight_half(nc, w_x2, s_x2, W2_words, W2_scales, 1, 0, (1, 0))
-        load_weight_half(nc, w_x2, s_x2, W2_words, W2_scales, 1, 1, (0, 1))
+            load_weight_half(nc, w_x1[h], s_x1[h], W2_words, W2_scales, 0, h, (0, 1), small[0])
+        small[0].append((b2_row[0:1, :], b2.rearrange("(x o) -> x o", x=1)))
+        load_weight_half(nc, w_even, s_even, W2_words, W2_scales, 1, 0, (0, 1), small[1])
+        load_weight_half(nc, w_even, s_even, W2_words, W2_scales, 1, 1, (1, 0), small[1])
+        sm, se = small[0], small[1]
+        x1_loads = [(x1_rows[:, p, :], x1[:, BLOCK * p : BLOCK * (p + 1), :]) for p in range(BLOCKS)]
+        pl = {n: block_pair_loads(n) for n in range(LOADS_AHEAD)}
+        go(*x1_loads[:2], *pl[0], *sm[:3], *se, *sm[6:], *x1_loads[2:], *sm[3:6])
         for n in range(1, LOADS_AHEAD):
-            load_block_pair(n)
-        w_x2_swapped = const.tile([P, 4 * CH], U8, align_bytes=64)
-        s_x2_swapped = const.tile([P, 2 * CH], U8, align_bytes=64)
-        for target, source, width in ((w_x2_swapped, w_x2, 2 * CH), (s_x2_swapped, s_x2, CH)):
+            go(*pl[n])
+        for target, source, width in ((w_odd, w_even, 2 * CH), (s_odd, s_even, CH)):
             nc.gpsimd.tensor_copy(out=target[:, 0:width].bitcast(I32), in_=source[:, width : 2 * width].bitcast(I32))
             nc.gpsimd.tensor_copy(out=target[:, width : 2 * width].bitcast(I32), in_=source[:, 0:width].bitcast(I32))
-        w_x2_by_order = (w_x2_swapped, w_x2)
-        s_x2_by_order = (s_x2_swapped, s_x2)
+        w_x2_by_order = (w_even, w_odd)
+        s_x2_by_order = (s_even, s_odd)
         warm = const.tile([P, 1], F32)
         nc.vector.memset(warm[:], 0.0)
         nc.scalar.activation(out=warm[:], in_=warm[:], func=SIGMOID)
 
-        x1_bank = flip_pool.tile([P, TILES_PER_BANK, 2, P], F32, tag="bank")
-        transpose_row_pairs(
-            nc,
-            x1_bank,
-            [x1_rows[:, 2 * s : 2 * s + 2, :].rearrange("c h k -> c (h k)").bitcast(F32) for s in range(2)],
-            identity,
-        )
-        b2_bank = acc_pool.tile([P, 2 * CH], F32, tag="acc")
-        nc.tensor.matmul(b2_bank[:, 0:CH], lhsT=ones[:], rhs=b2_row[:], start=True, stop=True)
         x1_grouped = const.tile([P, 2, P, 4], BF16, align_bytes=64)
-        nc.vector.tensor_copy(out=x1_grouped[:].bitcast(F32), in_=x1_bank[:].rearrange("n s u c -> n s c u"))
         x1_codes = const.tile([P, 2, P], U32, align_bytes=64)
         x1_plane = const.tile([P, 2, P], U8, align_bytes=64)
         rep_grouped = const.tile([P, 2 * BLOCK, P, 4], BF16, align_bytes=64)
@@ -294,23 +298,29 @@ def tile_differentiablelogicmachine_pa_t_kernel(tc, x1, x2, W2_words, W2_scales,
         rep_plane = const.tile([P, 2 * BLOCK, P], U8, align_bytes=64)
         b2_f32 = const.tile([P, CH], F32)
         own = const.tile([P, BLOCKS, 2 * CH], F32)
-        nc.vector.quantize_mx(
-            out=x1_codes[:].rearrange("n s c -> n (s c)").bitcast(FP8X4),
-            scales=x1_plane[:].rearrange("n s c -> n (s c)"),
-            in_=x1_grouped[:].rearrange("n s c t -> n (s c t)"),
-        )
-        nc.vector.tensor_copy(out=b2_f32[:], in_=b2_bank[:, 0:CH])
 
-        def repeat_rows(s):
+        def prepare_x1(s):
+            bank = flip_pool.tile([P, TILES_PER_BANK, 2, P], F32, tag="bank")
+            words = x1_rows[:, 2 * s : 2 * s + 2, :].rearrange("c h k -> c (h k)").bitcast(F32)
+            for u in range(2):
+                nc.tensor.transpose(bank[:, 0, u, :], words[:, u : 2 * WORDS : 2], identity[:])
+            nc.vector.tensor_copy(out=x1_grouped[:, s, :, :].bitcast(F32), in_=bank[:, 0, :, :].rearrange("n u c -> n c u"))
+            nc.vector.quantize_mx(
+                out=x1_codes[:, s, :].bitcast(FP8X4),
+                scales=x1_plane[:, s, :],
+                in_=x1_grouped[:, s, :, :].rearrange("n c t -> n (c t)"),
+            )
+
+        def repeat_rows(s, h):
             one = x1_grouped[:, s, :, :].bitcast(F32).rearrange("n (b a) u -> n b a u", a=BLOCK)
-            for d in range(BLOCK):
+            for d in range(4 * h, 4 * h + 4):
                 nc.scalar.copy(
                     out=rep_grouped[:, BLOCK * s + d, :, :].bitcast(F32).rearrange("n (b r) u -> n b r u", r=BLOCK),
                     in_=one[:, :, d : d + 1, :].to_broadcast([P, SCENES, BLOCK, 2]),
                 )
 
-        def quantise_repeated(s):
-            tiles = slice(BLOCK * s, BLOCK * (s + 1))
+        def quantise_repeated(s, h):
+            tiles = slice(BLOCK * s + 4 * h, BLOCK * s + 4 * h + 4)
             nc.vector.quantize_mx(
                 out=rep_codes[:, tiles, :].rearrange("n d c -> n (d c)").bitcast(FP8X4),
                 scales=rep_plane[:, tiles, :].rearrange("n d c -> n (d c)"),
@@ -331,30 +341,43 @@ def tile_differentiablelogicmachine_pa_t_kernel(tc, x1, x2, W2_words, W2_scales,
             nc.vector.tensor_tensor(out=own[:, p, 0:CH], in0=uv[:, CH : 2 * CH], in1=b2_f32[:], op=ADD)
             nc.vector.tensor_tensor(out=own[:, p, CH : 2 * CH], in0=uv[:, 0:CH], in1=b2_f32[:], op=ADD)
 
-        repeat_rows(0)
-        flip_block_pair(0)
+        steps = [(n, h) for n in range(count) for h in range(2)]
+        last = len(steps) - 1
+        prepare_x1(0)
+        repeat_rows(0, 0)
+        flip_half(*steps[0])
+        repeat_rows(0, 1)
+        b2_bank = acc_pool.tile([P, 2 * CH], F32, tag="acc")
+        nc.tensor.matmul(b2_bank[:, 0:CH], lhsT=ones[:], rhs=b2_row[:], start=True, stop=True)
+        nc.vector.tensor_copy(out=b2_f32[:], in_=b2_bank[:, 0:CH])
         make_own(0)
-        quantise_repeated(0)
-        quantise_block_pair(0)
-        flip_block_pair(1)
-
-        waiting = None
-        for n in range(count):
-            if n + LOADS_AHEAD < count:
-                load_block_pair(n + LOADS_AHEAD)
-            if n + 2 < count:
-                flip_block_pair(n + 2)
-            if n + 1 < count:
-                quantise_block_pair(n + 1)
-            if n == 0:
-                repeat_rows(1)
-            for d0 in range(0, BLOCK, TILES_PER_STEP):
-                multiply_step(n, d0)
-                if waiting is not None:
-                    finish_step(waiting[0], waiting[1])
-                waiting = (n, d0)
-            if n == 0:
-                quantise_repeated(1)
-            if n + 1 < BLOCKS:
-                make_own(n + 1)
-        finish_step(waiting[0], waiting[1])
+        quantise_repeated(0, 0)
+        for k in range(1, FLIP_AHEAD):
+            flip_half(*steps[k])
+        quantise_repeated(0, 1)
+        for k in range(QUANTISE_AHEAD):
+            quantise_half(*steps[k])
+        for k in range(len(steps)):
+            n, h = steps[k]
+            if h == 0 and n + LOADS_AHEAD < count:
+                for target, source in block_pair_loads(n + LOADS_AHEAD):
+                    nc.sync.dma_start(out=target, in_=source)
+            if k + FLIP_AHEAD <= last:
+                flip_half(*steps[k + FLIP_AHEAD])
+            if k + QUANTISE_AHEAD <= last:
+                quantise_half(*steps[k + QUANTISE_AHEAD])
+            if k == 0:
+                prepare_x1(1)
+                repeat_rows(1, 0)
+            if k == 1:
+                repeat_rows(1, 1)
+                quantise_repeated(1, 0)
+            if k == 2:
+                quantise_repeated(1, 1)
+            multiply_step(n, TILES_PER_STEP * h)
+            if k:
+                finish_step(steps[k - 1][0], TILES_PER_STEP * steps[k - 1][1])
+            if h and 0 < n < BLOCKS:
+                make_own(n)
+        for d0 in range(TILES_PER_STEP, BLOCK, END_TILES):
+            finish_step(count - 1, d0, END_TILES)

@@ -64,7 +64,7 @@ def transpose_row_pairs(nc, bank, row_pairs, identity):
 
 def tile_differentiablelogicmachine_pa_t_kernel(tc, x1, x2, W2_words, W2_scales, b2, out):
     nc = tc.nc
-    block_pairs = [(0, 0)] + [(p, q) for p in range(BLOCKS) for q in range(p + 1, BLOCKS)] + [(p, p) for p in range(1, BLOCKS)]
+    block_pairs = [(p, q) for p in range(BLOCKS) for q in range(p + 1, BLOCKS)] + [(p, p) for p in range(BLOCKS)]
     count = len(block_pairs)
 
     with tc.tile_pool(name="const", bufs=1) as const, tc.tile_pool(name="rows", bufs=count - BLOCKS) as rows_pool, tc.tile_pool(
@@ -76,6 +76,9 @@ def tile_differentiablelogicmachine_pa_t_kernel(tc, x1, x2, W2_words, W2_scales,
     ) as flip_pool, tc.psum_pool(name="acc", bufs=4) as acc_pool, tc.manual_schedule():
         x2_rows = {}
         x2_grouped = {}
+        x2_straight = {}
+        x2_straight_codes = {}
+        x2_straight_plane = {}
         x2_codes = {}
         x2_plane = {}
         results = {}
@@ -84,12 +87,10 @@ def tile_differentiablelogicmachine_pa_t_kernel(tc, x1, x2, W2_words, W2_scales,
             p, q = block_pairs[n]
             if p == q:
                 square = square_pool.tile([P, BLOCK + 1, CH], BF16)
+                nc.gpsimd.memset(square[:, BLOCK, :], 0.0)
                 own_rows = slice(BLOCK * p, BLOCK * (p + 1))
                 x2_rows[n] = square
-                return [
-                    (square[:, 1 : BLOCK + 1, :], x2[:, own_rows, own_rows, :]),
-                    (square[:, 0, :], x2[:, own_rows, BLOCK * (p + 1) - 1, :]),
-                ]
+                return [(square[:, 0:BLOCK, :], x2[:, own_rows, own_rows, :])]
             rows = rows_pool.tile([P, BLOCK, 2, CH], BF16)
             places = rows[:].rearrange("c d h k -> c (d h) k")
             i0, j0 = BLOCK * p, BLOCK * q
@@ -127,39 +128,46 @@ def tile_differentiablelogicmachine_pa_t_kernel(tc, x1, x2, W2_words, W2_scales,
                 )
 
         def flip_square_half(n, h):
-            grouped = x2_grouped[n]
+            mirrored = x2_grouped[n]
             words = x2_rows[n][:].rearrange("c y k -> c (y k)").bitcast(F32)
-            upper, lower = slice(0, HALF), slice(HALF, P)
-            by_tile = grouped[:].bitcast(F32)
+            if h == 0:
+                x2_straight[n] = quant_pool.tile([P, BLOCK // 2, P, 4], BF16, name="straight", align_bytes=64)
+            straight = x2_straight[n]
             for e in range(2 * h, 2 * h + 2):
                 bank = flip_pool.tile([P, TILES_PER_BANK, 2, P], F32, tag="bank")
                 transpose_row_pairs(
                     nc, bank, [words[:, WORDS * (2 * e + t) : WORDS * (2 * e + t + 2)] for t in range(TILES_PER_BANK)], identity
                 )
-                copy = nc.vector.tensor_copy if e % 2 else nc.scalar.copy
-                copy_mirrored = nc.vector.tensor_copy if e == 3 else nc.scalar.copy
-                as_it_is = bank[upper].rearrange("n t u c -> n t c u")
-                if e == 0:
-                    copy(out=by_tile[upper, BLOCK - 1, :, :], in_=as_it_is[:, 0, :, :])
-                    copy(out=by_tile[upper, 0, :, :], in_=as_it_is[:, 1, :, :])
-                else:
-                    copy(out=by_tile[upper, 2 * e - 1 : 2 * e + 1, :, :], in_=as_it_is)
-                copy_mirrored(
-                    out=by_tile[lower].rearrange("n d (b a) u -> n b d (a u)", a=BLOCK)[:, :, :, 4 * e : 4 * e + 4],
-                    in_=bank[lower].rearrange("n t u (b x) -> n b x (t u)", x=BLOCK),
+                nc.vector.tensor_copy(out=straight[:, e, :, :].bitcast(F32), in_=bank[:, 0, :, :].rearrange("n u c -> n c u"))
+                nc.scalar.copy(
+                    out=mirrored[:].bitcast(F32).rearrange("n d (b a) u -> n b d (a u)", a=BLOCK)[:, :, :, 4 * e : 4 * e + 4],
+                    in_=bank[:].rearrange("n t u (b x) -> n b x (t u)", x=BLOCK),
                 )
 
         def quantise_half(n, h):
+            if n in x2_straight and h == 0:
+                straight_codes = quant_pool.tile([P, BLOCK // 2, P], U32, align_bytes=64)
+                straight_plane = quant_pool.tile([P, BLOCK // 2, P], U8, align_bytes=64)
+                nc.vector.quantize_mx(
+                    out=straight_codes[:].rearrange("n d c -> n (d c)").bitcast(FP8X4),
+                    scales=straight_plane[:].rearrange("n d c -> n (d c)"),
+                    in_=x2_straight[n][:].rearrange("n d c t -> n (d c t)"),
+                )
+                x2_straight_codes[n] = straight_codes
+                x2_straight_plane[n] = straight_plane
             grouped = x2_grouped[n]
             if h == 0:
                 x2_codes[n] = quant_pool.tile([P, BLOCK, P], U32, name="codes", align_bytes=64)
                 x2_plane[n] = quant_pool.tile([P, BLOCK, P], U8, name="plane", align_bytes=64)
-            tiles = slice(TILES_PER_STEP * h, TILES_PER_STEP * (h + 1))
-            nc.vector.quantize_mx(
-                out=x2_codes[n][:, tiles, :].rearrange("n d c -> n (d c)").bitcast(FP8X4),
-                scales=x2_plane[n][:, tiles, :].rearrange("n d c -> n (d c)"),
-                in_=grouped[:, tiles, :, :].rearrange("n d c t -> n (d c t)"),
-            )
+            codes = x2_codes[n]
+            plane = x2_plane[n]
+            for d0 in (TILES_PER_STEP * h,):
+                tiles = slice(d0, d0 + TILES_PER_STEP)
+                nc.vector.quantize_mx(
+                    out=codes[:, tiles, :].rearrange("n d c -> n (d c)").bitcast(FP8X4),
+                    scales=plane[:, tiles, :].rearrange("n d c -> n (d c)"),
+                    in_=grouped[:, tiles, :, :].rearrange("n d c t -> n (d c t)"),
+                )
 
         def multiply_step(n, d0):
             p, q = block_pairs[n]
@@ -209,11 +217,20 @@ def tile_differentiablelogicmachine_pa_t_kernel(tc, x1, x2, W2_words, W2_scales,
                     x1_words = slice(2 * (CH + o0), 2 * (CH + o0) + CH)
                     nc.tensor.matmul_mx(
                         out=acc[:, c0 : c0 + CH // 2],
+                        lhsT=x2_straight_codes[n][:, e, :].bitcast(FP8X4),
+                        lhsT_scale=x2_straight_plane[n][:, e, :],
+                        rhs=w_straight[:, 2 * c0 : 2 * c0 + CH].bitcast(FP4X4),
+                        rhs_scale=s_straight[:, c0 : c0 + CH // 2],
+                        start=True,
+                        stop=False,
+                    )
+                    nc.tensor.matmul_mx(
+                        out=acc[:, c0 : c0 + CH // 2],
                         lhsT=x2_codes[n][:, d, :].bitcast(FP8X4),
                         lhsT_scale=x2_plane[n][:, d, :],
-                        rhs=w_even[:, words].bitcast(FP4X4),
-                        rhs_scale=s_even[:, cols],
-                        start=True,
+                        rhs=w_mirrored[:, words].bitcast(FP4X4),
+                        rhs_scale=s_mirrored[:, cols],
+                        start=False,
                         stop=False,
                     )
                     nc.tensor.matmul_mx(
@@ -262,6 +279,12 @@ def tile_differentiablelogicmachine_pa_t_kernel(tc, x1, x2, W2_words, W2_scales,
             nc.vector.memset(w_x1[h][:].bitcast(I32), 0)
             nc.vector.memset(s_x1[h][:].bitcast(I32), 0)
         nc.vector.memset(s_even[:].bitcast(I32), 0)
+        w_straight = const.tile([P, 4 * CH], U8, align_bytes=64)
+        s_straight = const.tile([P, 2 * CH], U8, align_bytes=64)
+        w_mirrored = const.tile([P, 2 * CH], U8, align_bytes=64)
+        s_mirrored = const.tile([P, CH], U8, align_bytes=64)
+        for zeroed in (w_straight, s_straight, w_mirrored, s_mirrored):
+            nc.gpsimd.memset(zeroed[:].bitcast(I32), 0)
         b2_row = const.tile([P, CH], BF16)
         nc.vector.memset(b2_row[:], 0.0)
         ones = const.tile([P, P], BF16)
@@ -278,12 +301,20 @@ def tile_differentiablelogicmachine_pa_t_kernel(tc, x1, x2, W2_words, W2_scales,
         sm, se = small[0], small[1]
         x1_loads = [(x1_rows[:, p, :], x1[:, BLOCK * p : BLOCK * (p + 1), :]) for p in range(BLOCKS)]
         pl = {n: block_pair_loads(n) for n in range(LOADS_AHEAD)}
-        go(*x1_loads[:2], *pl[0], *sm[:3], *se, *sm[6:], *x1_loads[2:], *sm[3:6])
+        go(*x1_loads[:2], *pl[0][:6], *sm[6:], *sm[:3], *pl[0][6:], *se, *sm[3:6], *x1_loads[2:])
         for n in range(1, LOADS_AHEAD):
             go(*pl[n])
         for target, source, width in ((w_odd, w_even, 2 * CH), (s_odd, s_even, CH)):
             nc.gpsimd.tensor_copy(out=target[:, 0:width].bitcast(I32), in_=source[:, width : 2 * width].bitcast(I32))
             nc.gpsimd.tensor_copy(out=target[:, width : 2 * width].bitcast(I32), in_=source[:, 0:width].bitcast(I32))
+        upper, lower = slice(0, HALF), slice(HALF, P)
+        for target, source, width in ((w_straight, w_even, 2 * CH), (s_straight, s_even, CH)):
+            nc.gpsimd.tensor_copy(out=target[upper, 0:width].bitcast(I32), in_=source[upper, 0:width].bitcast(I32))
+            nc.gpsimd.tensor_copy(
+                out=target[lower, width : 2 * width].bitcast(I32), in_=source[lower, width : 2 * width].bitcast(I32)
+            )
+        nc.gpsimd.tensor_copy(out=w_mirrored[upper, :].bitcast(I32), in_=w_even[upper, 2 * CH : 4 * CH].bitcast(I32))
+        nc.gpsimd.tensor_copy(out=s_mirrored[upper, :].bitcast(I32), in_=s_even[upper, CH : 2 * CH].bitcast(I32))
         w_x2_by_order = (w_even, w_odd)
         s_x2_by_order = (s_even, s_odd)
         warm = const.tile([P, 1], F32)

@@ -289,6 +289,8 @@ def tile_differentiablelogicmachine_pa_t_kernel(tc, x1, x2, W2_words, W2_scales,
         nc.vector.memset(b2_row[:], 0.0)
         ones = const.tile([P, P], BF16)
         nc.vector.memset(ones[:], 1.0)
+        idle = const.tile([P, 2 * CH], BF16)
+        nc.vector.memset(idle[:].bitcast(I32), 0)
         def go(*todo):
             for target, source in todo:
                 nc.sync.dma_start(out=target, in_=source)
@@ -329,6 +331,11 @@ def tile_differentiablelogicmachine_pa_t_kernel(tc, x1, x2, W2_words, W2_scales,
         rep_plane = const.tile([P, 2 * BLOCK, P], U8, align_bytes=64)
         b2_f32 = const.tile([P, CH], F32)
         own = const.tile([P, BLOCKS, 2 * CH], F32)
+
+        def keep_warm(times):
+            bank = acc_pool.tile([P, 2 * CH], F32, tag="acc")
+            for t in range(times):
+                nc.tensor.matmul(bank[:], lhsT=ones[:], rhs=idle[:], start=True, stop=True)
 
         def prepare_x1(s):
             bank = flip_pool.tile([P, TILES_PER_BANK, 2, P], F32, tag="bank")
@@ -374,10 +381,13 @@ def tile_differentiablelogicmachine_pa_t_kernel(tc, x1, x2, W2_words, W2_scales,
 
         steps = [(n, h) for n in range(count) for h in range(2)]
         last = len(steps) - 1
+        keep_warm(6)
         prepare_x1(0)
         repeat_rows(0, 0)
+        keep_warm(4)
         flip_half(*steps[0])
         repeat_rows(0, 1)
+        keep_warm(4)
         b2_bank = acc_pool.tile([P, 2 * CH], F32, tag="acc")
         nc.tensor.matmul(b2_bank[:, 0:CH], lhsT=ones[:], rhs=b2_row[:], start=True, stop=True)
         nc.vector.tensor_copy(out=b2_f32[:], in_=b2_bank[:, 0:CH])
@@ -385,6 +395,7 @@ def tile_differentiablelogicmachine_pa_t_kernel(tc, x1, x2, W2_words, W2_scales,
         quantise_repeated(0, 0)
         for k in range(1, FLIP_AHEAD):
             flip_half(*steps[k])
+            keep_warm(4)
         quantise_repeated(0, 1)
         for k in range(QUANTISE_AHEAD):
             quantise_half(*steps[k])

import concourse.mybir as mybir
from concourse.masks import make_identity

F32 = mybir.dt.float32
BF16 = mybir.dt.bfloat16
I32 = mybir.dt.int32
U32 = mybir.dt.uint32
U8 = mybir.dt.uint8
FP8X4 = mybir.dt.float8_e4m3fn_x4
FP4X4 = mybir.dt.float4_e2m1fn_x4
ADD = mybir.AluOpType.add
SIGMOID = mybir.ActivationFunctionType.Sigmoid

P = 128
SCENES = 16
OBJECTS = 32
CH = 256
HALF = 64
BLOCK = 8
BLOCKS = OBJECTS // BLOCK
WORDS = CH // 2
TILES_PER_BANK = 2
FLIP_AHEAD = 3
QUANTISE_AHEAD = 1
END_TILES = 2
TILES_PER_STEP = 4
LOADS_AHEAD = 5

FLOPS = 2 * SCENES * OBJECTS * OBJECTS * 4 * CH * CH


def load_weight_half(nc, words, plane, W2_words, W2_scales, source_half, half, groups, todo):
    rows = slice(HALF * source_half, HALF * (source_half + 1))
    to = slice(HALF * half, HALF * (half + 1))
    if groups == (0, 1):
        todo.append((words[to, :].bitcast(I32), W2_words[:, rows, :].bitcast(I32).rearrange("g p n -> p g n")))
    else:
        for side in range(2):
            todo.append(
                (words[to, 2 * CH * side : 2 * CH * (side + 1)].bitcast(I32), W2_words[groups[side], rows, :].bitcast(I32))
            )
    for quad in range(2):
        first = HALF * half + 32 * quad
        row = 8 * source_half + 4 * quad
        if groups == (0, 1):
            todo.append(
                (plane[first : first + 4, :].bitcast(I32), W2_scales[:, row : row + 4, :].bitcast(I32).rearrange("g r n -> r g n"))
            )
        else:
            for side in range(2):
                todo.append(
                    (
                        plane[first : first + 4, CH * side : CH * (side + 1)].bitcast(I32),
                        W2_scales[groups[side], row : row + 4, :].bitcast(I32),
                    )
                )


def transpose_row_pairs(nc, bank, row_pairs, identity):
    for t in range(TILES_PER_BANK):
        for u in range(2):
            nc.tensor.transpose(bank[:, t, u, :], row_pairs[t][:, u : 2 * WORDS : 2], identity[:])


def tile_differentiablelogicmachine_pa_t_kernel(tc, x1, x2, W2_words, W2_scales, b2, out):
    nc = tc.nc
    block_pairs = [(p, q) for p in range(BLOCKS) for q in range(p + 1, BLOCKS)] + [(p, p) for p in range(BLOCKS)]
    count = len(block_pairs)

    with tc.tile_pool(name="const", bufs=1) as const, tc.tile_pool(name="rows", bufs=count - BLOCKS) as rows_pool, tc.tile_pool(
        name="square", bufs=BLOCKS
    ) as square_pool, tc.tile_pool(
        name="quant", bufs=2
    ) as quant_pool, tc.tile_pool(name="result", bufs=4) as result_pool, tc.psum_pool(
        name="flip", bufs=4
    ) as flip_pool, tc.psum_pool(name="acc", bufs=4) as acc_pool, tc.manual_schedule():
        x2_rows = {}
        x2_grouped = {}
        x2_straight = {}
        x2_straight_codes = {}
        x2_straight_plane = {}
        x2_codes = {}
        x2_plane = {}
        results = {}

        def block_pair_loads(n):
            p, q = block_pairs[n]
            if p == q:
                square = square_pool.tile([P, BLOCK + 1, CH], BF16)
                nc.gpsimd.memset(square[:, BLOCK, :], 0.0)
                own_rows = slice(BLOCK * p, BLOCK * (p + 1))
                x2_rows[n] = square
                return [(square[:, 0:BLOCK, :], x2[:, own_rows, own_rows, :])]
            rows = rows_pool.tile([P, BLOCK, 2, CH], BF16)
            places = rows[:].rearrange("c d h k -> c (d h) k")
            i0, j0 = BLOCK * p, BLOCK * q
            todo = []
            for d in range(0, BLOCK, 2):
                todo.append((places[:, 2 * d, :], x2[:, j0 + d, i0 : i0 + BLOCK, :]))
                todo.append((places[:, 2 * d + 1 : 2 * d + 3, :], x2[:, i0 : i0 + BLOCK, j0 + d : j0 + d + 2, :]))
                todo.append((places[:, 2 * d + 3, :], x2[:, j0 + d + 1, i0 : i0 + BLOCK, :]))
            x2_rows[n] = rows
            return todo

        def load_block_pair(n):
            for target, source in block_pair_loads(n):
                nc.sync.dma_start(out=target, in_=source)

        def flip_half(n, h):
            if h == 0:
                x2_grouped[n] = quant_pool.tile([P, BLOCK, P, 4], BF16, name="grouped", align_bytes=64)
            grouped = x2_grouped[n]
            if block_pairs[n][0] == block_pairs[n][1]:
                flip_square_half(n, h)
                return
            rows = x2_rows[n]
            for d0 in range(TILES_PER_STEP * h, TILES_PER_STEP * (h + 1), TILES_PER_BANK):
                bank = flip_pool.tile([P, TILES_PER_BANK, 2, P], F32, tag="bank")
                transpose_row_pairs(
                    nc,
                    bank,
                    [rows[:, d0 + t, :, :].rearrange("c h k -> c (h k)").bitcast(F32) for t in range(TILES_PER_BANK)],
                    identity,
                )
                nc.scalar.copy(
                    out=grouped[:, d0 : d0 + TILES_PER_BANK, :, :].bitcast(F32),
                    in_=bank[:].rearrange("n t u c -> n t c u"),
                )

        def flip_square_half(n, h):
            mirrored = x2_grouped[n]
            words = x2_rows[n][:].rearrange("c y k -> c (y k)").bitcast(F32)
            if h == 0:
                x2_straight[n] = quant_pool.tile([P, BLOCK // 2, P, 4], BF16, name="straight", align_bytes=64)
            straight = x2_straight[n]
            for e in range(2 * h, 2 * h + 2):
                bank = flip_pool.tile([P, TILES_PER_BANK, 2, P], F32, tag="bank")
                transpose_row_pairs(
                    nc, bank, [words[:, WORDS * (2 * e + t) : WORDS * (2 * e + t + 2)] for t in range(TILES_PER_BANK)], identity
                )
                nc.vector.tensor_copy(out=straight[:, e, :, :].bitcast(F32), in_=bank[:, 0, :, :].rearrange("n u c -> n c u"))
                nc.scalar.copy(
                    out=mirrored[:].bitcast(F32).rearrange("n d (b a) u -> n b d (a u)", a=BLOCK)[:, :, :, 4 * e : 4 * e + 4],
                    in_=bank[:].rearrange("n t u (b x) -> n b x (t u)", x=BLOCK),
                )

        def quantise_half(n, h):
            if n in x2_straight and h == 0:
                straight_codes = quant_pool.tile([P, BLOCK // 2, P], U32, align_bytes=64)
                straight_plane = quant_pool.tile([P, BLOCK // 2, P], U8, align_bytes=64)
                nc.vector.quantize_mx(
                    out=straight_codes[:].rearrange("n d c -> n (d c)").bitcast(FP8X4),
                    scales=straight_plane[:].rearrange("n d c -> n (d c)"),
                    in_=x2_straight[n][:].rearrange("n d c t -> n (d c t)"),
                )
                x2_straight_codes[n] = straight_codes
                x2_straight_plane[n] = straight_plane
            grouped = x2_grouped[n]
            if h == 0:
                x2_codes[n] = quant_pool.tile([P, BLOCK, P], U32, name="codes", align_bytes=64)
                x2_plane[n] = quant_pool.tile([P, BLOCK, P], U8, name="plane", align_bytes=64)
            codes = x2_codes[n]
            plane = x2_plane[n]
            for d0 in (TILES_PER_STEP * h,):
                tiles = slice(d0, d0 + TILES_PER_STEP)
                nc.vector.quantize_mx(
                    out=codes[:, tiles, :].rearrange("n d c -> n (d c)").bitcast(FP8X4),
                    scales=plane[:, tiles, :].rearrange("n d c -> n (d c)"),
                    in_=grouped[:, tiles, :, :].rearrange("n d c t -> n (d c t)"),
                )

        def multiply_step(n, d0):
            p, q = block_pairs[n]
            if d0 == 0:
                result = result_pool.tile([P, 2, BLOCK, CH], F32)
                results[n] = result
            if p == q:
                multiply_square(n, d0)
                return
            for d in range(d0, d0 + TILES_PER_STEP):
                acc = acc_pool.tile([P, 2 * CH], F32, tag="acc")
                nc.tensor.matmul_mx(
                    out=acc[:],
                    lhsT=x2_codes[n][:, d, :].bitcast(FP8X4),
                    lhsT_scale=x2_plane[n][:, d, :],
                    rhs=w_x2_by_order[d % 2][:].bitcast(FP4X4),
                    rhs_scale=s_x2_by_order[d % 2][:],
                    start=True,
                    stop=False,
                )
                nc.tensor.matmul_mx(
                    out=acc[:],
                    lhsT=rep_codes[:, BLOCK * (q // 2) + d, :].bitcast(FP8X4),
                    lhsT_scale=rep_plane[:, BLOCK * (q // 2) + d, :],
                    rhs=w_x1[q % 2][:].bitcast(FP4X4),
                    rhs_scale=s_x1[q % 2][:],
                    start=False,
                    stop=True,
                )
                nc.vector.tensor_tensor(
                    out=results[n][:, :, d, :],
                    in0=acc[:].rearrange("c (s o) -> c s o", o=CH),
                    in1=own[:, p, :].rearrange("c (s o) -> c s o", o=CH),
                    op=ADD,
                )

        def multiply_square(n, d0):
            p = block_pairs[n][0]
            for e in range(d0 // 2, (d0 + TILES_PER_STEP) // 2):
                acc = acc_pool.tile([P, 2 * CH], F32, tag="acc")
                for c0 in range(0, 2 * CH, CH // 2):
                    d = 2 * e + c0 // CH
                    o0 = c0 % CH
                    cols = slice(o0, o0 + CH // 2)
                    words = slice(2 * o0, 2 * o0 + CH)
                    x1_cols = slice(CH + o0, CH + o0 + CH // 2)
                    x1_words = slice(2 * (CH + o0), 2 * (CH + o0) + CH)
                    nc.tensor.matmul_mx(
                        out=acc[:, c0 : c0 + CH // 2],
                        lhsT=x2_straight_codes[n][:, e, :].bitcast(FP8X4),
                        lhsT_scale=x2_straight_plane[n][:, e, :],
                        rhs=w_straight[:, 2 * c0 : 2 * c0 + CH].bitcast(FP4X4),
                        rhs_scale=s_straight[:, c0 : c0 + CH // 2],
                        start=True,
                        stop=False,
                    )
                    nc.tensor.matmul_mx(
                        out=acc[:, c0 : c0 + CH // 2],
                        lhsT=x2_codes[n][:, d, :].bitcast(FP8X4),
                        lhsT_scale=x2_plane[n][:, d, :],
                        rhs=w_mirrored[:, words].bitcast(FP4X4),
                        rhs_scale=s_mirrored[:, cols],
                        start=False,
                        stop=False,
                    )
                    nc.tensor.matmul_mx(
                        out=acc[:, c0 : c0 + CH // 2],
                        lhsT=rep_codes[:, BLOCK * (p // 2) + d, :].bitcast(FP8X4),
                        lhsT_scale=rep_plane[:, BLOCK * (p // 2) + d, :],
                        rhs=w_x1[p % 2][:, x1_words].bitcast(FP4X4),
                        rhs_scale=s_x1[p % 2][:, x1_cols],
                        start=False,
                        stop=True,
                    )
                nc.vector.tensor_tensor(
                    out=results[n][:, 1, 2 * e : 2 * e + 2, :],
                    in0=acc[:].rearrange("c (s o) -> c s o", o=CH),
                    in1=own[:, p : p + 1, CH : 2 * CH].to_broadcast([P, 2, CH]),
                    op=ADD,
                )

        def finish_step(n, d0, tiles=TILES_PER_STEP):
            p, q = block_pairs[n]
            first = 0 if q > p else 1
            i0, j0 = BLOCK * p, BLOCK * q
            d1 = d0 + tiles
            done = results[n][:, first:2, d0:d1, :]
            nc.scalar.activation(out=done, in_=done, func=SIGMOID)
            nc.sync.dma_start(
                out=out[:, i0 : i0 + BLOCK, j0 + d0 : j0 + d1, :].rearrange("b a j o -> b a (j o)"),
                in_=results[n][:, 1, d0:d1, :].rearrange("c j o -> c (j o)"),
            )
            if q > p:
                for d in range(d0, d1):
                    nc.sync.dma_start(out=out[:, j0 + d, i0 : i0 + BLOCK, :], in_=results[n][:, 0, d, :])

        identity = const.tile([P, P], F32)
        make_identity(nc, identity[:])

        x1_rows = const.tile([P, BLOCKS, CH], BF16)

        w_even = const.tile([P, 4 * CH], U8, align_bytes=64)
        s_even = const.tile([P, 2 * CH], U8, align_bytes=64)
        w_odd = const.tile([P, 4 * CH], U8, align_bytes=64)
        s_odd = const.tile([P, 2 * CH], U8, align_bytes=64)
        w_x1 = [const.tile([P, 4 * CH], U8, name="w_x1_%d" % h, align_bytes=64) for h in range(2)]
        s_x1 = [const.tile([P, 2 * CH], U8, name="s_x1_%d" % h, align_bytes=64) for h in range(2)]
        for h in range(2):
            nc.vector.memset(w_x1[h][:].bitcast(I32), 0)
            nc.vector.memset(s_x1[h][:].bitcast(I32), 0)
        nc.vector.memset(s_even[:].bitcast(I32), 0)
        w_straight = const.tile([P, 4 * CH], U8, align_bytes=64)
        s_straight = const.tile([P, 2 * CH], U8, align_bytes=64)
        w_mirrored = const.tile([P, 2 * CH], U8, align_bytes=64)
        s_mirrored = const.tile([P, CH], U8, align_bytes=64)
        for zeroed in (w_straight, s_straight, w_mirrored, s_mirrored):
            nc.gpsimd.memset(zeroed[:].bitcast(I32), 0)
        b2_row = const.tile([P, CH], BF16)
        nc.vector.memset(b2_row[:], 0.0)
        ones = const.tile([P, P], BF16)
        nc.vector.memset(ones[:], 1.0)
        idle = const.tile([P, 2 * CH], BF16)
        nc.vector.memset(idle[:].bitcast(I32), 0)
        def go(*todo):
            for target, source in todo:
                nc.sync.dma_start(out=target, in_=source)
        small = [[], []]
        for h in range(2):
            load_weight_half(nc, w_x1[h], s_x1[h], W2_words, W2_scales, 0, h, (0, 1), small[0])
        small[0].append((b2_row[0:1, :], b2.rearrange("(x o) -> x o", x=1)))
        load_weight_half(nc, w_even, s_even, W2_words, W2_scales, 1, 0, (0, 1), small[1])
        load_weight_half(nc, w_even, s_even, W2_words, W2_scales, 1, 1, (1, 0), small[1])
        sm, se = small[0], small[1]
        x1_loads = [(x1_rows[:, p, :], x1[:, BLOCK * p : BLOCK * (p + 1), :]) for p in range(BLOCKS)]
        pl = {n: block_pair_loads(n) for n in range(LOADS_AHEAD)}
        go(*x1_loads[:2], *pl[0][:6], *sm[6:], *sm[:3], *pl[0][6:], *se, *sm[3:6], *x1_loads[2:])
        for n in range(1, LOADS_AHEAD):
            go(*pl[n])
        for target, source, width in ((w_odd, w_even, 2 * CH), (s_odd, s_even, CH)):
            nc.gpsimd.tensor_copy(out=target[:, 0:width].bitcast(I32), in_=source[:, width : 2 * width].bitcast(I32))
            nc.gpsimd.tensor_copy(out=target[:, width : 2 * width].bitcast(I32), in_=source[:, 0:width].bitcast(I32))
        upper, lower = slice(0, HALF), slice(HALF, P)
        for target, source, width in ((w_straight, w_even, 2 * CH), (s_straight, s_even, CH)):
            nc.gpsimd.tensor_copy(out=target[upper, 0:width].bitcast(I32), in_=source[upper, 0:width].bitcast(I32))
            nc.gpsimd.tensor_copy(
                out=target[lower, width : 2 * width].bitcast(I32), in_=source[lower, width : 2 * width].bitcast(I32)
            )
        nc.gpsimd.tensor_copy(out=w_mirrored[upper, :].bitcast(I32), in_=w_even[upper, 2 * CH : 4 * CH].bitcast(I32))
        nc.gpsimd.tensor_copy(out=s_mirrored[upper, :].bitcast(I32), in_=s_even[upper, CH : 2 * CH].bitcast(I32))
        w_x2_by_order = (w_even, w_odd)
        s_x2_by_order = (s_even, s_odd)
        warm = const.tile([P, 1], F32)
        nc.vector.memset(warm[:], 0.0)
        nc.scalar.activation(out=warm[:], in_=warm[:], func=SIGMOID)

        x1_grouped = const.tile([P, 2, P, 4], BF16, align_bytes=64)
        x1_codes = const.tile([P, 2, P], U32, align_bytes=64)
        x1_plane = const.tile([P, 2, P], U8, align_bytes=64)
        rep_grouped = const.tile([P, 2 * BLOCK, P, 4], BF16, align_bytes=64)
        rep_codes = const.tile([P, 2 * BLOCK, P], U32, align_bytes=64)
        rep_plane = const.tile([P, 2 * BLOCK, P], U8, align_bytes=64)
        b2_f32 = const.tile([P, CH], F32)
        own = const.tile([P, BLOCKS, 2 * CH], F32)

        def keep_warm(times):
            bank = acc_pool.tile([P, 2 * CH], F32, tag="acc")
            for t in range(times):
                nc.tensor.matmul(bank[:], lhsT=ones[:], rhs=idle[:], start=True, stop=True)

        def prepare_x1(s):
            bank = flip_pool.tile([P, TILES_PER_BANK, 2, P], F32, tag="bank")
            words = x1_rows[:, 2 * s : 2 * s + 2, :].rearrange("c h k -> c (h k)").bitcast(F32)
            for u in range(2):
                nc.tensor.transpose(bank[:, 0, u, :], words[:, u : 2 * WORDS : 2], identity[:])
            nc.vector.tensor_copy(out=x1_grouped[:, s, :, :].bitcast(F32), in_=bank[:, 0, :, :].rearrange("n u c -> n c u"))
            nc.vector.quantize_mx(
                out=x1_codes[:, s, :].bitcast(FP8X4),
                scales=x1_plane[:, s, :],
                in_=x1_grouped[:, s, :, :].rearrange("n c t -> n (c t)"),
            )

        def repeat_rows(s, h):
            one = x1_grouped[:, s, :, :].bitcast(F32).rearrange("n (b a) u -> n b a u", a=BLOCK)
            for d in range(4 * h, 4 * h + 4):
                nc.scalar.copy(
                    out=rep_grouped[:, BLOCK * s + d, :, :].bitcast(F32).rearrange("n (b r) u -> n b r u", r=BLOCK),
                    in_=one[:, :, d : d + 1, :].to_broadcast([P, SCENES, BLOCK, 2]),
                )

        def quantise_repeated(s, h):
            tiles = slice(BLOCK * s + 4 * h, BLOCK * s + 4 * h + 4)
            nc.vector.quantize_mx(
                out=rep_codes[:, tiles, :].rearrange("n d c -> n (d c)").bitcast(FP8X4),
                scales=rep_plane[:, tiles, :].rearrange("n d c -> n (d c)"),
                in_=rep_grouped[:, tiles, :, :].rearrange("n d c t -> n (d c t)"),
            )

        def make_own(p):
            uv = acc_pool.tile([P, 2 * CH], F32, tag="acc")
            nc.tensor.matmul_mx(
                out=uv[:],
                lhsT=x1_codes[:, p // 2, :].bitcast(FP8X4),
                lhsT_scale=x1_plane[:, p // 2, :],
                rhs=w_x1[p % 2][:].bitcast(FP4X4),
                rhs_scale=s_x1[p % 2][:],
                start=True,
                stop=True,
            )
            nc.vector.tensor_tensor(out=own[:, p, 0:CH], in0=uv[:, CH : 2 * CH], in1=b2_f32[:], op=ADD)
            nc.vector.tensor_tensor(out=own[:, p, CH : 2 * CH], in0=uv[:, 0:CH], in1=b2_f32[:], op=ADD)

        steps = [(n, h) for n in range(count) for h in range(2)]
        last = len(steps) - 1
        keep_warm(6)
        prepare_x1(0)
        repeat_rows(0, 0)
        keep_warm(4)
        flip_half(*steps[0])
        repeat_rows(0, 1)
        keep_warm(4)
        b2_bank = acc_pool.tile([P, 2 * CH], F32, tag="acc")
        nc.tensor.matmul(b2_bank[:, 0:CH], lhsT=ones[:], rhs=b2_row[:], start=True, stop=True)
        nc.vector.tensor_copy(out=b2_f32[:], in_=b2_bank[:, 0:CH])
        make_own(0)
        quantise_repeated(0, 0)
        for k in range(1, FLIP_AHEAD):
            flip_half(*steps[k])
            keep_warm(4)
        quantise_repeated(0, 1)
        for k in range(QUANTISE_AHEAD):
            quantise_half(*steps[k])
        for k in range(len(steps)):
            n, h = steps[k]
            if h == 0 and n + LOADS_AHEAD < count:
                for target, source in block_pair_loads(n + LOADS_AHEAD):
                    nc.sync.dma_start(out=target, in_=source)
            if k + FLIP_AHEAD <= last:
                flip_half(*steps[k + FLIP_AHEAD])
            if k + QUANTISE_AHEAD <= last:
                quantise_half(*steps[k + QUANTISE_AHEAD])
            if k == 0:
                prepare_x1(1)
                repeat_rows(1, 0)
            if k == 1:
                repeat_rows(1, 1)
                quantise_repeated(1, 0)
            if k == 2:
                quantise_repeated(1, 1)
            multiply_step(n, TILES_PER_STEP * h)
            if k:
                finish_step(steps[k - 1][0], TILES_PER_STEP * steps[k - 1][1])
            if h and 0 < n < BLOCKS:
                make_own(n)
        for d0 in range(TILES_PER_STEP, BLOCK, END_TILES):
            finish_step(count - 1, d0, END_TILES)
